import numpy as np
import ml_dtypes


def mxq(x, axis, fmt="e4m3"):
    dtype, down = {"e4m3": (ml_dtypes.float8_e4m3fn, 7), "e5m2": (ml_dtypes.float8_e5m2, 14)}[fmt]
    v = np.moveaxis(np.asarray(x, np.float32).astype(ml_dtypes.bfloat16).astype(np.float64), axis, -1)
    blocks = v.reshape(v.shape[:-1] + (-1, 32))
    amax = np.abs(blocks).max(-1, keepdims=True)
    byte = np.maximum(np.where(amax > 0, np.frexp(amax)[1] - 1 + 127, 0) - down, 1)
    scale = np.exp2(byte - 127.0)
    codes = (blocks / scale).astype(np.float32).astype(dtype).astype(np.float64)
    return np.moveaxis((codes * scale).reshape(v.shape), -1, axis)


WIDE = False


def mx_kscale(k):
    if not WIDE:
        return np.ones(k)
    levels = np.array([10, -10, 5, -5, 0])
    if k % 512:
        return np.exp2(np.random.permutation(np.resize(levels, k // 32))).repeat(32)
    a = np.empty((k // 512, 16))
    for p in range(k // 512):
        a[p, :8] = np.random.permutation(np.resize(levels, 8))
        for g in range(8):
            far = levels[np.abs(levels - a[p, g]) >= 10]
            a[p, g + 8] = far[np.random.randint(len(far))]
    return np.exp2(a.ravel()).repeat(32)


BF16 = ml_dtypes.bfloat16


def bf(x):
    return np.asarray(x, np.float32).astype(BF16)


def f64(x):
    return np.asarray(x).astype(np.float64)


B, T, D, NH, N_MLP = 4, 1024, 512, 16, 512
LN_EPS = 1e-6


def layer_norm(v, g, b):
    mu = v.mean(-1, keepdims=True)
    var = np.square(v - mu).mean(-1, keepdims=True)
    return (v - mu) / np.sqrt(var + LN_EPS) * g + b


def erf(v):
    z = np.clip(v, -6.0, 6.0)
    r = 2.0 * z * z
    term = z.copy()
    total = z.copy()
    for n in range(1, 120):
        term = term * r / (2.0 * n + 1.0)
        total = total + term
    return 2.0 / np.sqrt(np.pi) * np.exp(-z * z) * total


def gelu_erf(v):
    return 0.5 * v * (1.0 + erf(v / np.sqrt(2.0)))


def draw0():
    s, t = mx_kscale(D), mx_kscale(D)
    return {"attn_out": bf(np.random.standard_normal((B, T, D)) * 0.25 * s),
            "x": bf(np.random.standard_normal((B, T, D)) * 1.5 + np.random.standard_normal((B, T, 1)) * 0.5),
            "W_proj": bf(np.random.standard_normal((D, D)) * 3.0 / np.sqrt(D) / s),
            "b_proj": bf(np.random.standard_normal(D) * 0.2),
            "g2": bf((1.0 + 0.1 * np.random.standard_normal(D)) * t),
            "beta2": bf(0.1 * np.random.standard_normal(D) * t),
            "W1": bf(np.random.standard_normal((N_MLP, D)) / np.sqrt(D) / t),
            "b1": bf(np.random.standard_normal(N_MLP) * 0.2)}


def core(attn_out, x, W_proj, b_proj, g2, beta2, W1, b1):
    o = (mxq(f64(attn_out), 2, "e4m3") @ mxq(f64(W_proj), 1, "e4m3").T) + f64(b_proj)
    x_mid = f64(x) + o
    h = layer_norm(x_mid, f64(g2), f64(beta2))
    u = gelu_erf((mxq(h, 2, "e4m3") @ mxq(f64(W1), 1, "e4m3").T) + f64(b1))
    return x_mid, u


def e4m3fn_bytes(y):
    return np.clip(np.asarray(y, np.float64), -448.0, 448.0).astype(np.float32).astype(ml_dtypes.float8_e4m3fn).view(np.uint8)


def e4m3fn_values(b):
    return np.asarray(b, np.uint8).view(ml_dtypes.float8_e4m3fn).astype(np.float64)


def setup_inputs():
    d = draw0()
    x0 = np.asarray(d['attn_out']).astype(np.float64)
    s = (np.max(np.abs(x0), axis=(0, 1), keepdims=True) / 448.0).astype(np.float32)
    out = {}
    for k, v in d.items():
        if k == 'attn_out':
            out['attn_out_bytes'] = e4m3fn_bytes(x0 / s.astype(np.float64))
            out['attn_out_scale'] = s
        else:
            out[k] = v
    return out


def reference(attn_out_bytes, attn_out_scale, x, W_proj, b_proj, g2, beta2, W1, b1):
    return core(e4m3fn_values(attn_out_bytes) * attn_out_scale.astype(np.float64), x, W_proj, b_proj, g2, beta2, W1, b1)

@@ -1,0 +1,401 @@
+from contextlib import ExitStack
+
+import concourse.mybir as mybir
+from concourse.masks import make_identity
+
+TOKENS, D, N_MLP = 4096, 512, 512
+FLOPS = 2 * TOKENS * D * (D + N_MLP)
+LN_EPS = 1e-6
+
+F32 = mybir.dt.float32
+BF16 = mybir.dt.bfloat16
+U32 = mybir.dt.uint32
+U8 = mybir.dt.uint8
+FP8 = mybir.dt.float8_e4m3fn
+FP8X4 = mybir.dt.float8_e4m3fn_x4
+ACT = mybir.ActivationFunctionType
+ALU = mybir.AluOpType
+
+P = 128
+R = TOKENS // P
+A = 2
+G = R // A
+CHUNKS = [1, 1, 2, 4, 4, 4]
+
+
+def tile_block_pb_t_kernel(
+    tc, attn_out_bytes, attn_out_scale, x, W_proj, b_proj, g2, beta2, W1, b1, out_0, out_1
+):
+    nc = tc.nc
+    bytes_hbm = attn_out_bytes.rearrange("b s d -> (b s) d").rearrange("(p r) d -> p (r d)", p=P)
+    x_hbm = x.rearrange("b s d -> (b s) d").rearrange("(p r) d -> p (r d)", p=P)
+    xm_hbm = out_0.rearrange("b s d -> (b s) d").rearrange("(p r) d -> p (r d)", p=P)
+    u_hbm = out_1.rearrange("b s d -> (b s) d").rearrange("(p r) d -> p (r d)", p=P)
+
+    with ExitStack() as ctx:
+        keep = ctx.enter_context(tc.tile_pool(name="keep", bufs=1))
+        work = ctx.enter_context(tc.tile_pool(name="work", bufs=3))
+        psum = ctx.enter_context(tc.psum_pool(name="psum", bufs=2))
+        ctx.enter_context(tc.manual_schedule())
+
+        scale = keep.tile([P, D], F32, name="scale")
+        nc.scalar.dma_start(out=scale[:], in_=attn_out_scale.rearrange("a b k -> (a b k)").partition_broadcast(P))
+        dummy = keep.tile([P, 1], F32, name="dummy")
+        nc.vector.memset(dummy[:], 0.0)
+        vrows = keep.tile([P, D], BF16, name="vrows")
+        nc.vector.memset(vrows[:], 0.0)
+        grows = keep.tile([P, P], BF16, name="grows")
+        nc.vector.memset(grows[:], 0.0)
+        neghalf = keep.tile([P, A], F32, name="neghalf")
+        nc.vector.memset(neghalf[:], -0.5)
+        ident = keep.tile([P, P], F32, name="ident")
+        make_identity(nc, ident[:])
+        identb = keep.tile([P, P], BF16, name="identb")
+        nc.vector.tensor_copy(out=identb[:], in_=ident[:])
+        nc.scalar.activation(out=dummy[:], in_=dummy[:], func=ACT.Gelu)
+
+        starts = [sum(CHUNKS[:i]) for i in range(len(CHUNKS))]
+        byte_tiles = []
+        x_tiles = []
+        for i in range(len(CHUNKS)):
+            w = CHUNKS[i] * A * D
+            bt = keep.tile([P, w], U8, name="bytes%d" % i, align_bytes=64)
+            byte_tiles.append(bt)
+            xt = keep.tile([P, w], BF16, name="xin%d" % i, align_bytes=64)
+            x_tiles.append(xt)
+
+        def load_bytes(i):
+            c0 = starts[i] * A * D
+            nc.sync.dma_start(out=byte_tiles[i][:], in_=bytes_hbm[:, c0 : c0 + CHUNKS[i] * A * D])
+
+        def load_x(i):
+            c0 = starts[i] * A * D
+            nc.sync.dma_start(out=x_tiles[i][:], in_=x_hbm[:, c0 : c0 + CHUNKS[i] * A * D])
+
+        def where(g, a):
+            i = max(j for j in range(len(CHUNKS)) if starts[j] <= g)
+            c0 = ((g - starts[i]) * A + a) * D
+            return i, slice(c0, c0 + D)
+
+        wp = keep.tile([P, 4, D], BF16, name="wp")
+        w1 = keep.tile([P, 4, D], BF16, name="w1")
+        wp_hbm = W_proj.rearrange("(c p) k -> p c k", p=P)
+        w1_hbm = W1.rearrange("(c p) k -> p c k", p=P)
+        load_bytes(0)
+        nc.sync.dma_start(out=wp[:, 0:2, :], in_=wp_hbm[:, 0:2, :])
+        nc.sync.dma_start(out=wp[:, 2:4, :], in_=wp_hbm[:, 2:4, :])
+        nc.scalar.dma_start(out=vrows[0:1, :], in_=b_proj.rearrange("(o k) -> o k", o=1))
+        nc.scalar.dma_start(out=vrows[1:2, :], in_=b1.rearrange("(o k) -> o k", o=1))
+        nc.scalar.dma_start(
+            out=grows[0:4, :].rearrange("t (b q) -> t b q", q=8), in_=g2.rearrange("(b t q) -> t b q", t=4, q=8)
+        )
+        nc.scalar.dma_start(
+            out=grows[4:8, :].rearrange("t (b q) -> t b q", q=8), in_=beta2.rearrange("(b t q) -> t b q", t=4, q=8)
+        )
+        load_x(0)
+        load_bytes(1)
+        load_x(1)
+        nc.sync.dma_start(out=w1[:], in_=w1_hbm)
+        for i in range(2, len(CHUNKS)):
+            load_bytes(i)
+            load_x(i)
+
+        T = {}
+
+        def st_P(g):
+            ab = work.tile([P, A, D], BF16, name="ab", align_bytes=64)
+            T["ab", g] = ab
+            for a in range(A):
+                i, cols = where(g, a)
+                nc.vector.tensor_tensor(
+                    out=ab[:, a, :], in0=byte_tiles[i][:, cols].bitcast(FP8), in1=scale[:], op=ALU.mult
+                )
+
+        def st_TA(g):
+            ta = psum.tile([P, A, 2, P], F32, name="ta")
+            T["ta", g] = ta
+            for a in range(A):
+                words = T["ab", g][:, a, :].bitcast(F32)
+                for u in range(2):
+                    nc.tensor.transpose(ta[:, a, u, :], words[:, u::2], ident[:])
+
+        def st_CA(g):
+            ag = work.tile([P, A, P, 4], BF16, name="ag", align_bytes=64)
+            T["ag", g] = ag
+            nc.scalar.copy(
+                out=ag[:].rearrange("p a r f -> p a (r f)").bitcast(F32).rearrange("p a (r u) -> p a r u", u=2),
+                in_=T["ta", g][:].rearrange("p a u r -> p a r u"),
+            )
+
+        def st_QA(g):
+            ac = work.tile([P, A * P], U32, name="ac", align_bytes=64)
+            asc = work.tile([P, A * P], U8, name="asc", align_bytes=64)
+            T["ac", g] = (ac, asc)
+            nc.vector.quantize_mx(
+                out=ac[:].bitcast(FP8X4), scales=asc[:], in_=T["ag", g][:].rearrange("p a r f -> p (a r f)")
+            )
+
+        def mx(tag, codes, w, a):
+            acc = psum.tile([P, 512], F32, name=tag)
+            nc.tensor.matmul_mx(
+                out=acc[:],
+                lhsT=codes[0][:, a * P : (a + 1) * P].bitcast(FP8X4),
+                lhsT_scale=codes[1][:, a * P : (a + 1) * P],
+                rhs=w[0][:].bitcast(FP8X4),
+                rhs_scale=w[1][:],
+                start=True,
+                stop=True,
+            )
+            return acc
+
+        def st_M1(g):
+            T["m1", g] = [mx("m1", T["ac", g], T["wp"], a) for a in range(A)]
+
+        def st_XB(g, a):
+            if a == 0:
+                xb = work.tile([P, A, D], F32, name="xb")
+                T["xb", g] = xb
+            i, cols = where(g, a)
+            nc.gpsimd.tensor_tensor(out=T["xb", g][:, a, :], in0=x_tiles[i][:, cols], in1=bp[:], op=ALU.add)
+
+        def st_XA(g):
+            xm = work.tile([P, A, D], F32, name="xm", bufs=4)
+            sums = work.tile([P, A], F32, name="sums")
+            T["xm", g] = xm
+            T["sums", g] = sums
+            for a in range(A):
+                nc.vector.scalar_tensor_tensor(
+                    out=xm[:, a, :],
+                    in0=T["m1", g][a][:],
+                    scalar=1.0,
+                    in1=T["xb", g][:, a, :],
+                    op0=ALU.mult,
+                    op1=ALU.add,
+                    accum_out=sums[:, a : a + 1],
+                )
+            nc.sync.dma_start(out=xm_hbm[:, g * A * D : (g + 1) * A * D], in_=xm[:].rearrange("p a d -> p (a d)"))
+
+        def st_NM(g):
+            nm = work.tile([P, A], F32, name="nm")
+            T["nm", g] = nm
+            nc.gpsimd.tensor_scalar(
+                out=nm[:], in0=T["sums", g][:], scalar1=-1.0 / D, scalar2=0.0, op0=ALU.mult, op1=ALU.add
+            )
+
+        def st_SQ(g):
+            ss = work.tile([P, A], F32, name="ss")
+            T["ss", g] = ss
+            for a in range(A):
+                junk = work.tile([P, D], BF16, name="junk")
+                nc.scalar.activation(
+                    out=junk[:],
+                    in_=T["xm", g][:, a, :],
+                    func=ACT.Square,
+                    bias=T["nm", g][:, a : a + 1],
+                    accum_out=ss[:, a : a + 1],
+                )
+
+        def st_RS(g):
+            var = work.tile([P, A], F32, name="var")
+            rstd = work.tile([P, A], F32, name="rstd")
+            nmr = work.tile([P, A], F32, name="nmr")
+            T["rstd", g] = rstd
+            T["nmr", g] = nmr
+            nc.gpsimd.tensor_scalar(
+                out=var[:], in0=T["ss", g][:], scalar1=1.0 / D, scalar2=LN_EPS, op0=ALU.mult, op1=ALU.add
+            )
+            nc.gpsimd.tensor_tensor(out=rstd[:], in0=var[:], in1=neghalf[:], op=ALU.pow)
+            nc.gpsimd.tensor_tensor(out=nmr[:], in0=T["nm", g][:], in1=rstd[:], op=ALU.mult)
+
+        def st_Z(g):
+            z = work.tile([P, A, D], F32, name="z", bufs=2)
+            T["z", g] = z
+            for a in range(A):
+                src = T["xm", g][:, a, :].rearrange("p (b t q) -> p t b q", t=4, q=8)
+                dst = z[:, a, :].rearrange("p (t b q) -> p t b q", t=4, q=8)
+                if a == 1 and g % 2 == 0:
+                    nc.vector.tensor_scalar(
+                        out=dst,
+                        in0=src,
+                        scalar1=T["nm", g][:, a : a + 1],
+                        scalar2=T["rstd", g][:, a : a + 1],
+                        op0=ALU.add,
+                        op1=ALU.mult,
+                    )
+                else:
+                    nc.scalar.activation(
+                        out=dst,
+                        in_=src,
+                        func=ACT.Identity,
+                        scale=T["rstd", g][:, a : a + 1],
+                        bias=T["nmr", g][:, a : a + 1],
+                    )
+
+        def st_TZ(g):
+            za = psum.tile([P, 2, A * P], F32, name="za", bufs=1)
+            zb = psum.tile([P, 2, A * P], F32, name="zb", bufs=1)
+            T["zp", g] = (za, zb)
+            for a in range(A):
+                for t in range(4):
+                    nc.tensor.transpose(
+                        T["zp", g][t // 2][:, t % 2, a * P : (a + 1) * P],
+                        T["z", g][:, a, t * P : (t + 1) * P],
+                        ident[:],
+                    )
+
+        def st_PL(g):
+            hp = work.tile([P, 4, A * P], BF16, name="hp")
+            T["hp", g] = hp
+            for t in range(4):
+                nc.scalar.activation(
+                    out=hp[:, t, :],
+                    in_=T["zp", g][t // 2][:, t % 2, :],
+                    func=ACT.Identity,
+                    scale=gcols[:, t : t + 1],
+                    bias=gcols[:, 4 + t : 5 + t],
+                )
+
+        def st_IL(g):
+            hg = work.tile([P, A * P, 4], BF16, name="hg", align_bytes=64)
+            T["hg", g] = hg
+            nc.vector.tensor_copy(
+                out=hg[:].rearrange("p (c i) t -> p c t i", i=4),
+                in_=T["hp", g][:].rearrange("p t (c i) -> p c t i", i=4),
+            )
+
+        def st_QH(g):
+            hc = work.tile([P, A * P], U32, name="hc", align_bytes=64)
+            hsc = work.tile([P, A * P], U8, name="hsc", align_bytes=64)
+            T["hc", g] = (hc, hsc)
+            nc.vector.quantize_mx(
+                out=hc[:].bitcast(FP8X4), scales=hsc[:], in_=T["hg", g][:].rearrange("p r t -> p (r t)")
+            )
+
+        def st_M2(g):
+            T["m2", g] = [mx("m2", T["hc", g], T["w1"], a) for a in range(A)]
+
+        def st_B1(g, a):
+            if a == 0:
+                v = work.tile([P, A, N_MLP], F32, name="v", bufs=2)
+                T["v", g] = v
+            nc.vector.tensor_tensor(out=T["v", g][:, a, :], in0=T["m2", g][a][:], in1=b1f[:], op=ALU.add)
+
+        def st_GE(g):
+            u = work.tile([P, A * N_MLP], F32, name="u")
+            nc.scalar.activation(out=u[:], in_=T["v", g][:].rearrange("p a n -> p (a n)"), func=ACT.Gelu)
+            nc.sync.dma_start(out=u_hbm[:, g * A * N_MLP : (g + 1) * A * N_MLP], in_=u[:])
+
+        def iteration(k):
+            def has(g):
+                return 0 <= g < G
+
+            if has(k - 1):
+                st_Z(k - 1)
+            if has(k + 1):
+                st_XB(k + 1, 0)
+            if has(k):
+                st_XA(k)
+                st_NM(k)
+            if has(k + 1):
+                st_XB(k + 1, 1)
+            if has(k - 1):
+                st_TZ(k - 1)
+            if has(k - 4):
+                st_GE(k - 4)
+            if has(k - 3):
+                st_M2(k - 3)
+            if has(k + 1):
+                st_QA(k + 1)
+                st_M1(k + 1)
+            if has(k):
+                st_SQ(k)
+                st_RS(k)
+            if has(k + 2):
+                st_P(k + 2)
+                st_TA(k + 2)
+            if has(k - 2):
+                st_IL(k - 2)
+            if has(k - 3):
+                st_B1(k - 3, 0)
+            if has(k - 2):
+                st_QH(k - 2)
+            if has(k - 3):
+                st_B1(k - 3, 1)
+            if has(k - 1):
+                st_PL(k - 1)
+            if has(k + 2):
+                st_CA(k + 2)
+
+        wps = []
+        for h in range(2):
+            wpp = psum.tile([P, 2, 2, P], F32, name="za" if h == 0 else "zb", bufs=1)
+            wps.append(wpp)
+            for c in range(2):
+                words = wp[:, 2 * h + c, :].bitcast(F32)
+                for e in range(2):
+                    nc.tensor.transpose(wpp[:, c, e, :], words[:, e::2], ident[:])
+        st_P(0)
+        st_TA(0)
+        wpg = keep.tile([P, D, 4], BF16, name="wpg", align_bytes=64)
+        for h in range(2):
+            dst = (
+                wpg[:, h * 2 * P : (h + 1) * 2 * P, :]
+                .rearrange("p n t -> p (n t)")
+                .bitcast(F32)
+                .rearrange("p (c n e) -> p c n e", c=2, e=2)
+            )
+            src = wps[h][:].rearrange("p c e n -> p c n e")
+            if h == 0:
+                nc.vector.tensor_copy(out=dst, in_=src)
+            else:
+                nc.scalar.copy(out=dst, in_=src)
+        st_CA(0)
+        wpc = keep.tile([P, D], U32, name="wpc", align_bytes=64)
+        wpsc = keep.tile([P, D], U8, name="wpsc", align_bytes=64)
+        T["wp"] = (wpc, wpsc)
+        st_QA(0)
+        nc.vector.quantize_mx(out=wpc[:].bitcast(FP8X4), scales=wpsc[:], in_=wpg[:].rearrange("p n t -> p (n t)"))
+        bp = keep.tile([P, D], F32, name="bp")
+        b1f = keep.tile([P, D], F32, name="b1f")
+        for r in range(2):
+            bb = psum.tile([P, 512], F32, name="m2")
+            nc.tensor.matmul(
+                out=bb[:], lhsT=identb[:, r : r + 1].to_broadcast([P, P]), rhs=vrows[:], start=True, stop=True
+            )
+            nc.scalar.copy(out=bp[:] if r == 0 else b1f[:], in_=bb[:])
+        gp = psum.tile([P, P], BF16, name="m2")
+        nc.tensor.transpose(gp[:], grows[:], identb[:])
+        gcols = keep.tile([P, 8], F32, name="gcols")
+        nc.scalar.copy(out=gcols[:], in_=gp[:, 0:8])
+        st_XB(0, 0)
+        st_XB(0, 1)
+        st_M1(0)
+        st_P(1)
+        st_TA(1)
+        st_CA(1)
+        iteration(0)
+        w1p = keep.tile([P, 4, D], BF16, name="w1p")
+        w1g = keep.tile([P, N_MLP, 4], BF16, name="w1g", align_bytes=64)
+        for c in range(4):
+            nc.vector.tensor_copy(
+                out=w1p[:, c, :].rearrange("p (t b q) -> p t b q", t=4, q=8),
+                in_=w1[:, c, :].rearrange("p (b t q) -> p t b q", t=4, q=8),
+            )
+        for h in range(2):
+            w1t = psum.tile([P, 2, 4, P], BF16, name="m2")
+            for c in range(2):
+                for t in range(4):
+                    nc.tensor.transpose(w1t[:, c, t, :], w1p[:, 2 * h + c, t * P : (t + 1) * P], identb[:])
+            dst = w1g[:, h * 2 * P : (h + 1) * 2 * P, :].rearrange("p (c n) t -> p c n t", c=2)
+            src = w1t[:].rearrange("p c t n -> p c n t")
+            if h == 0:
+                nc.vector.tensor_copy(out=dst, in_=src)
+            else:
+                nc.scalar.copy(out=dst, in_=src)
+        w1c = keep.tile([P, N_MLP], U32, name="w1c", align_bytes=64)
+        w1sc = keep.tile([P, N_MLP], U8, name="w1sc", align_bytes=64)
+        T["w1"] = (w1c, w1sc)
+        nc.vector.quantize_mx(out=w1c[:].bitcast(FP8X4), scales=w1sc[:], in_=w1g[:].rearrange("p n t -> p (n t)"))
+
+        for k in range(1, G + 4):
+            iteration(k)

@@ -38,8 +38,8 @@ def tile_block_pb_t_kernel(
         psum = ctx.enter_context(tc.psum_pool(name="psum", bufs=2))
         ctx.enter_context(tc.manual_schedule())
 
-        scale = keep.tile([P, D], F32, name="scale")
-        nc.scalar.dma_start(out=scale[:], in_=attn_out_scale.rearrange("a b k -> (a b k)").partition_broadcast(P))
+        scale = keep.tile([P, A * D], F32, name="scale")
+        nc.scalar.dma_start(out=scale[:, 0:D], in_=attn_out_scale.rearrange("a b k -> (a b k)").partition_broadcast(P))
         dummy = keep.tile([P, 1], F32, name="dummy")
         nc.vector.memset(dummy[:], 0.0)
         vrows = keep.tile([P, D], BF16, name="vrows")
@@ -84,16 +84,16 @@ def tile_block_pb_t_kernel(
         load_bytes(0)
         nc.sync.dma_start(out=wp[:, 0:2, :], in_=wp_hbm[:, 0:2, :])
         nc.sync.dma_start(out=wp[:, 2:4, :], in_=wp_hbm[:, 2:4, :])
-        nc.scalar.dma_start(out=vrows[0:1, :], in_=b_proj.rearrange("(o k) -> o k", o=1))
-        nc.scalar.dma_start(out=vrows[1:2, :], in_=b1.rearrange("(o k) -> o k", o=1))
         nc.scalar.dma_start(
             out=grows[0:4, :].rearrange("t (b q) -> t b q", q=8), in_=g2.rearrange("(b t q) -> t b q", t=4, q=8)
         )
         nc.scalar.dma_start(
             out=grows[4:8, :].rearrange("t (b q) -> t b q", q=8), in_=beta2.rearrange("(b t q) -> t b q", t=4, q=8)
         )
-        load_x(0)
+        nc.scalar.dma_start(out=grows[8:12, :], in_=b_proj.rearrange("(f p) -> f p", p=P))
+        nc.scalar.dma_start(out=vrows[0:1, :], in_=b1.rearrange("(o k) -> o k", o=1))
         load_bytes(1)
+        load_x(0)
         load_x(1)
         nc.sync.dma_start(out=w1[:], in_=w1_hbm)
         for i in range(2, len(CHUNKS)):
@@ -103,19 +103,23 @@ def tile_block_pb_t_kernel(
         T = {}
 
         def st_P(g):
-            ab = work.tile([P, A, D], BF16, name="ab", align_bytes=64)
+            ab = work.tile([P, A * D], BF16, name="ab", align_bytes=64)
             T["ab", g] = ab
-            for a in range(A):
-                i, cols = where(g, a)
+            i, first = where(g, 0)
+            c0 = first.start
+            for lo, hi in [(0, D), (D, A * D)] if g == 0 else [(0, A * D)]:
                 nc.vector.tensor_tensor(
-                    out=ab[:, a, :], in0=byte_tiles[i][:, cols].bitcast(FP8), in1=scale[:], op=ALU.mult
+                    out=ab[:, lo:hi],
+                    in0=byte_tiles[i][:, c0 + lo : c0 + hi].bitcast(FP8),
+                    in1=scale[:, 0 : hi - lo],
+                    op=ALU.mult,
                 )
 
         def st_TA(g):
-            ta = psum.tile([P, A, 2, P], F32, name="ta")
+            ta = psum.tile([P, A, 2, P], F32, name="ta", tag="mm")
             T["ta", g] = ta
             for a in range(A):
-                words = T["ab", g][:, a, :].bitcast(F32)
+                words = T["ab", g][:, a * D : (a + 1) * D].bitcast(F32)
                 for u in range(2):
                     nc.tensor.transpose(ta[:, a, u, :], words[:, u::2], ident[:])
 
@@ -135,28 +139,41 @@ def tile_block_pb_t_kernel(
                 out=ac[:].bitcast(FP8X4), scales=asc[:], in_=T["ag", g][:].rearrange("p a r f -> p (a r f)")
             )
 
-        def mx(tag, codes, w, a):
-            acc = psum.tile([P, 512], F32, name=tag)
-            nc.tensor.matmul_mx(
-                out=acc[:],
-                lhsT=codes[0][:, a * P : (a + 1) * P].bitcast(FP8X4),
-                lhsT_scale=codes[1][:, a * P : (a + 1) * P],
-                rhs=w[0][:].bitcast(FP8X4),
-                rhs_scale=w[1][:],
-                start=True,
-                stop=True,
-            )
-            return acc
-
         def st_M1(g):
-            T["m1", g] = [mx("m1", T["ac", g], T["wp"], a) for a in range(A)]
+            ma = psum.tile([P, 2, A * P], F32, name="ma", bufs=1)
+            mb = psum.tile([P, 2, A * P], F32, name="mb", bufs=1)
+            T["m1", g] = (ma, mb)
+            for f in range(4):
+                nc.tensor.matmul_mx(
+                    out=T["m1", g][f // 2][:, f % 2, :],
+                    lhsT=wpc[:, f * P : (f + 1) * P].bitcast(FP8X4),
+                    lhsT_scale=wpsc[:, f * P : (f + 1) * P],
+                    rhs=T["ac", g][0][:].bitcast(FP8X4),
+                    rhs_scale=T["ac", g][1][:],
+                    start=True,
+                    stop=True,
+                )
 
-        def st_XB(g, a):
-            if a == 0:
-                xb = work.tile([P, A, D], F32, name="xb")
-                T["xb", g] = xb
-            i, cols = where(g, a)
-            nc.gpsimd.tensor_tensor(out=T["xb", g][:, a, :], in0=x_tiles[i][:, cols], in1=bp[:], op=ALU.add)
+        def st_OT(g):
+            ot = work.tile([P, 4, A * P], F32, name="ot", bufs=2)
+            T["ot", g] = ot
+            for f in range(4):
+                nc.scalar.activation(
+                    out=ot[:, f, :],
+                    in_=T["m1", g][f // 2][:, f % 2, :],
+                    func=ACT.Identity,
+                    bias=gcols[:, 8 + f : 9 + f],
+                )
+
+        def st_TO(g):
+            t0 = psum.tile([P, D], F32, name="t0", bufs=1)
+            t1 = psum.tile([P, D], F32, name="t1", bufs=1)
+            T["to", g] = (t0, t1)
+            for a in range(A):
+                for f in range(4):
+                    nc.tensor.transpose(
+                        T["to", g][a][:, f * P : (f + 1) * P], T["ot", g][:, f, a * P : (a + 1) * P], ident[:]
+                    )
 
         def st_XA(g):
             xm = work.tile([P, A, D], F32, name="xm", bufs=4)
@@ -164,11 +181,12 @@ def tile_block_pb_t_kernel(
             T["xm", g] = xm
             T["sums", g] = sums
             for a in range(A):
+                i, cols = where(g, a)
                 nc.vector.scalar_tensor_tensor(
                     out=xm[:, a, :],
-                    in0=T["m1", g][a][:],
+                    in0=T["to", g][a][:],
                     scalar=1.0,
-                    in1=T["xb", g][:, a, :],
+                    in1=x_tiles[i][:, cols],
                     op0=ALU.mult,
                     op1=ALU.add,
                     accum_out=sums[:, a : a + 1],
@@ -191,21 +209,19 @@ def tile_block_pb_t_kernel(
                     out=junk[:],
                     in_=T["xm", g][:, a, :],
                     func=ACT.Square,
-                    bias=T["nm", g][:, a : a + 1],
+                    scale=-float(D),
+                    bias=T["sums", g][:, a : a + 1],
                     accum_out=ss[:, a : a + 1],
                 )
 
         def st_RS(g):
             var = work.tile([P, A], F32, name="var")
             rstd = work.tile([P, A], F32, name="rstd")
-            nmr = work.tile([P, A], F32, name="nmr")
             T["rstd", g] = rstd
-            T["nmr", g] = nmr
             nc.gpsimd.tensor_scalar(
-                out=var[:], in0=T["ss", g][:], scalar1=1.0 / D, scalar2=LN_EPS, op0=ALU.mult, op1=ALU.add
+                out=var[:], in0=T["ss", g][:], scalar1=1.0 / D**3, scalar2=LN_EPS, op0=ALU.mult, op1=ALU.add
             )
             nc.gpsimd.tensor_tensor(out=rstd[:], in0=var[:], in1=neghalf[:], op=ALU.pow)
-            nc.gpsimd.tensor_tensor(out=nmr[:], in0=T["nm", g][:], in1=rstd[:], op=ALU.mult)
 
         def st_Z(g):
             z = work.tile([P, A, D], F32, name="z", bufs=2)
@@ -213,27 +229,18 @@ def tile_block_pb_t_kernel(
             for a in range(A):
                 src = T["xm", g][:, a, :].rearrange("p (b t q) -> p t b q", t=4, q=8)
                 dst = z[:, a, :].rearrange("p (t b q) -> p t b q", t=4, q=8)
-                if a == 1 and g % 2 == 0:
-                    nc.vector.tensor_scalar(
-                        out=dst,
-                        in0=src,
-                        scalar1=T["nm", g][:, a : a + 1],
-                        scalar2=T["rstd", g][:, a : a + 1],
-                        op0=ALU.add,
-                        op1=ALU.mult,
-                    )
-                else:
-                    nc.scalar.activation(
-                        out=dst,
-                        in_=src,
-                        func=ACT.Identity,
-                        scale=T["rstd", g][:, a : a + 1],
-                        bias=T["nmr", g][:, a : a + 1],
-                    )
+                nc.vector.tensor_scalar(
+                    out=dst,
+                    in0=src,
+                    scalar1=T["nm", g][:, a : a + 1],
+                    scalar2=T["rstd", g][:, a : a + 1],
+                    op0=ALU.add,
+                    op1=ALU.mult,
+                )
 
         def st_TZ(g):
-            za = psum.tile([P, 2, A * P], F32, name="za", bufs=1)
-            zb = psum.tile([P, 2, A * P], F32, name="zb", bufs=1)
+            za = psum.tile([P, 2, A * P], F32, name="za", tag="za", bufs=1)
+            zb = psum.tile([P, 2, A * P], F32, name="zb", tag="zb", bufs=1)
             T["zp", g] = (za, zb)
             for a in range(A):
                 for t in range(4):
@@ -247,6 +254,16 @@ def tile_block_pb_t_kernel(
             hp = work.tile([P, 4, A * P], BF16, name="hp")
             T["hp", g] = hp
             for t in range(4):
+                if g == G - 1 and t < 2:
+                    nc.vector.tensor_scalar(
+                        out=hp[:, t, :],
+                        in0=T["zp", g][t // 2][:, t % 2, :],
+                        scalar1=gcols[:, t : t + 1],
+                        scalar2=gcols[:, 4 + t : 5 + t],
+                        op0=ALU.mult,
+                        op1=ALU.add,
+                    )
+                    continue
                 nc.scalar.activation(
                     out=hp[:, t, :],
                     in_=T["zp", g][t // 2][:, t % 2, :],
@@ -272,7 +289,20 @@ def tile_block_pb_t_kernel(
             )
 
         def st_M2(g):
-            T["m2", g] = [mx("m2", T["hc", g], T["w1"], a) for a in range(A)]
+            accs = []
+            for a in range(A):
+                acc = psum.tile([P, N_MLP], F32, name="acc", tag="mm")
+                nc.tensor.matmul_mx(
+                    out=acc[:],
+                    lhsT=T["hc", g][0][:, a * P : (a + 1) * P].bitcast(FP8X4),
+                    lhsT_scale=T["hc", g][1][:, a * P : (a + 1) * P],
+                    rhs=w1c[:].bitcast(FP8X4),
+                    rhs_scale=w1sc[:],
+                    start=True,
+                    stop=True,
+                )
+                accs.append(acc)
+            T["m2", g] = accs
 
         def st_B1(g, a):
             if a == 0:
@@ -289,53 +319,51 @@ def tile_block_pb_t_kernel(
             def has(g):
                 return 0 <= g < G
 
-            if has(k - 1):
-                st_Z(k - 1)
-            if has(k + 1):
-                st_XB(k + 1, 0)
+            if has(k + 2):
+                st_CA(k + 2)
+            if has(k - 3):
+                st_M2(k - 3)
             if has(k):
                 st_XA(k)
                 st_NM(k)
-            if has(k + 1):
-                st_XB(k + 1, 1)
             if has(k - 1):
+                st_Z(k - 1)
                 st_TZ(k - 1)
-            if has(k - 4):
-                st_GE(k - 4)
-            if has(k - 3):
-                st_M2(k - 3)
             if has(k + 1):
-                st_QA(k + 1)
-                st_M1(k + 1)
+                st_OT(k + 1)
+                st_TO(k + 1)
             if has(k):
                 st_SQ(k)
                 st_RS(k)
-            if has(k + 2):
-                st_P(k + 2)
-                st_TA(k + 2)
-            if has(k - 2):
-                st_IL(k - 2)
             if has(k - 3):
                 st_B1(k - 3, 0)
-            if has(k - 2):
-                st_QH(k - 2)
+            if has(k + 2):
+                st_QA(k + 2)
+                st_M1(k + 2)
             if has(k - 3):
                 st_B1(k - 3, 1)
             if has(k - 1):
                 st_PL(k - 1)
-            if has(k + 2):
-                st_CA(k + 2)
+            if has(k - 2):
+                st_IL(k - 2)
+            if has(k + 3):
+                st_P(k + 3)
+                st_TA(k + 3)
+            if has(k - 2):
+                st_QH(k - 2)
+            if has(k - 3):
+                st_GE(k - 3)
 
         wps = []
         for h in range(2):
-            wpp = psum.tile([P, 2, 2, P], F32, name="za" if h == 0 else "zb", bufs=1)
+            wpp = psum.tile([P, 2, 2, P], F32, name="wpp", tag="za" if h == 0 else "zb", bufs=1)
             wps.append(wpp)
             for c in range(2):
                 words = wp[:, 2 * h + c, :].bitcast(F32)
                 for e in range(2):
                     nc.tensor.transpose(wpp[:, c, e, :], words[:, e::2], ident[:])
-        st_P(0)
-        st_TA(0)
+        iteration(-3)
+        nc.vector.tensor_copy(out=scale[:, D : 2 * D], in_=scale[:, 0:D])
         wpg = keep.tile([P, D, 4], BF16, name="wpg", align_bytes=64)
         for h in range(2):
             dst = (
@@ -349,30 +377,19 @@ def tile_block_pb_t_kernel(
                 nc.vector.tensor_copy(out=dst, in_=src)
             else:
                 nc.scalar.copy(out=dst, in_=src)
-        st_CA(0)
         wpc = keep.tile([P, D], U32, name="wpc", align_bytes=64)
         wpsc = keep.tile([P, D], U8, name="wpsc", align_bytes=64)
-        T["wp"] = (wpc, wpsc)
-        st_QA(0)
         nc.vector.quantize_mx(out=wpc[:].bitcast(FP8X4), scales=wpsc[:], in_=wpg[:].rearrange("p n t -> p (n t)"))
-        bp = keep.tile([P, D], F32, name="bp")
-        b1f = keep.tile([P, D], F32, name="b1f")
-        for r in range(2):
-            bb = psum.tile([P, 512], F32, name="m2")
-            nc.tensor.matmul(
-                out=bb[:], lhsT=identb[:, r : r + 1].to_broadcast([P, P]), rhs=vrows[:], start=True, stop=True
-            )
-            nc.scalar.copy(out=bp[:] if r == 0 else b1f[:], in_=bb[:])
-        gp = psum.tile([P, P], BF16, name="m2")
+        gp = psum.tile([P, P], BF16, name="gp", tag="za", bufs=1)
         nc.tensor.transpose(gp[:], grows[:], identb[:])
-        gcols = keep.tile([P, 8], F32, name="gcols")
-        nc.scalar.copy(out=gcols[:], in_=gp[:, 0:8])
-        st_XB(0, 0)
-        st_XB(0, 1)
-        st_M1(0)
-        st_P(1)
-        st_TA(1)
-        st_CA(1)
+        gcols = keep.tile([P, 12], F32, name="gcols")
+        nc.scalar.copy(out=gcols[:], in_=gp[:, 0:12])
+        bb = psum.tile([P, N_MLP], F32, name="bb", tag="zb", bufs=1)
+        nc.tensor.matmul(out=bb[:], lhsT=identb[:, 0:1].to_broadcast([P, P]), rhs=vrows[:], start=True, stop=True)
+        b1f = keep.tile([P, N_MLP], F32, name="b1f")
+        nc.scalar.copy(out=b1f[:], in_=bb[:])
+        iteration(-2)
+        iteration(-1)
         iteration(0)
         w1p = keep.tile([P, 4, D], BF16, name="w1p")
         w1g = keep.tile([P, N_MLP, 4], BF16, name="w1g", align_bytes=64)
@@ -382,7 +399,7 @@ def tile_block_pb_t_kernel(
                 in_=w1[:, c, :].rearrange("p (b t q) -> p t b q", t=4, q=8),
             )
         for h in range(2):
-            w1t = psum.tile([P, 2, 4, P], BF16, name="m2")
+            w1t = psum.tile([P, 2, 4, P], BF16, name="w1t", tag="za" if h == 0 else "zb", bufs=1)
             for c in range(2):
                 for t in range(4):
                     nc.tensor.transpose(w1t[:, c, t, :], w1p[:, 2 * h + c, t * P : (t + 1) * P], identb[:])
@@ -394,7 +411,6 @@ def tile_block_pb_t_kernel(
                 nc.scalar.copy(out=dst, in_=src)
         w1c = keep.tile([P, N_MLP], U32, name="w1c", align_bytes=64)
         w1sc = keep.tile([P, N_MLP], U8, name="w1sc", align_bytes=64)
-        T["w1"] = (w1c, w1sc)
         nc.vector.quantize_mx(out=w1c[:].bitcast(FP8X4), scales=w1sc[:], in_=w1g[:].rearrange("p n t -> p (n t)"))
 
         for k in range(1, G + 4):

@@ -21,6 +21,13 @@ R = TOKENS // P
 A = 2
 G = R // A
 CHUNKS = [1, 1, 2, 4, 4, 4]
+ORDER = [('CA', 3), ('M1', 2), ('XA0', 0), ('OT', 1), ('XA1', 0), ('Z0', -1), ('IL', -2), ('M20', -3), ('Z1', -1), ('M21', -3), ('QH', -2), ('SQ', 0), ('NM', 0), ('QA', 3), ('P', 4), ('DZ', -1), ('TZ0', -1), ('B10', -3), ('B11', -3), ('RS', 0), ('TZ1', -1), ('PL', -1), ('TO', 1), ('TA', 4), ('GE', -3)]
+HEAD = [('P', 0), ('WPT', 0), ('TA', 0), ('CA', 0), ('SC', 0), ('P', 1), ('WPT', 1), ('QA', 0), ('WPC', 1), ('TA', 1), ('WPC', 0), ('W1P', 1), ('W1P', 0), ('GC', 0), ('P', 3), ('WPQ', 0), ('CA', 1), ('M1', 0), ('P', 2), ('OT', 0), ('TA', 2), ('W1P', 3), ('TO', 0), ('QA', 1), ('P', 4), ('XA0', 0), ('M1', 1), ('OT', 1), ('BB', 0), ('W1P', 2), ('XA1', 0), ('TA', 3), ('CA', 2), ('CA', 3), ('NM', 0), ('W1T', 0), ('QA', 2), ('W1C', 0), ('W1T', 1), ('SQ', 0), ('W1C', 1), ('M1', 2), ('RS', 0), ('QA', 3), ('TO', 1), ('TA', 4), ('W1Q', 0)]
+TAIL = {16: [('Z0', -1), ('M20', -3), ('Z1', -1), ('IL', -2), ('B10', -3), ('M21', -3), ('QH', -2), ('TZ0', -1), ('B11', -3), ('TZ1', -1), ('PL', -1), ('GE', -3)], 17: [('M20', -3), ('B10', -3), ('IL', -2), ('M21', -3), ('B11', -3), ('GE', -3), ('QH', -2)], 18: [('M20', -3), ('B10', -3), ('M21', -3), ('B11', -3), ('GE', -3)]}
+KFIRST = 1
+PL_V = {13,11,5}
+OT_V = {11,14,7,3,0,1}
+PBUFS = 5
 
 
 def tile_block_pb_t_kernel(
@@ -40,12 +47,14 @@ def tile_block_pb_t_kernel(
 
         scale = keep.tile([P, A * D], F32, name="scale")
         nc.scalar.dma_start(out=scale[:, 0:D], in_=attn_out_scale.rearrange("a b k -> (a b k)").partition_broadcast(P))
-        dummy = keep.tile([P, 1], F32, name="dummy")
-        nc.vector.memset(dummy[:], 0.0)
         vrows = keep.tile([P, D], BF16, name="vrows")
         nc.vector.memset(vrows[:], 0.0)
         grows = keep.tile([P, P], BF16, name="grows")
         nc.vector.memset(grows[:], 0.0)
+        dummy = keep.tile([P, 1], F32, name="dummy")
+        nc.vector.memset(dummy[:], 0.0)
+        epsc = keep.tile([P, 1], F32, name="epsc")
+        nc.vector.tensor_scalar(out=epsc[:], in0=dummy[:], scalar1=LN_EPS, scalar2=None, op0=ALU.add)
         neghalf = keep.tile([P, A], F32, name="neghalf")
         nc.vector.memset(neghalf[:], -0.5)
         ident = keep.tile([P, P], F32, name="ident")
@@ -84,14 +93,14 @@ def tile_block_pb_t_kernel(
         load_bytes(0)
         nc.sync.dma_start(out=wp[:, 0:2, :], in_=wp_hbm[:, 0:2, :])
         nc.sync.dma_start(out=wp[:, 2:4, :], in_=wp_hbm[:, 2:4, :])
-        nc.scalar.dma_start(
+        nc.sync.dma_start(
             out=grows[0:4, :].rearrange("t (b q) -> t b q", q=8), in_=g2.rearrange("(b t q) -> t b q", t=4, q=8)
         )
-        nc.scalar.dma_start(
+        nc.sync.dma_start(
             out=grows[4:8, :].rearrange("t (b q) -> t b q", q=8), in_=beta2.rearrange("(b t q) -> t b q", t=4, q=8)
         )
-        nc.scalar.dma_start(out=grows[8:12, :], in_=b_proj.rearrange("(f p) -> f p", p=P))
-        nc.scalar.dma_start(out=vrows[0:1, :], in_=b1.rearrange("(o k) -> o k", o=1))
+        nc.sync.dma_start(out=grows[8:12, :], in_=b_proj.rearrange("(f p) -> f p", p=P))
+        nc.sync.dma_start(out=vrows[0:1, :], in_=b1.rearrange("(o k) -> o k", o=1))
         load_bytes(1)
         load_x(0)
         load_x(1)
@@ -103,7 +112,7 @@ def tile_block_pb_t_kernel(
         T = {}
 
         def st_P(g):
-            ab = work.tile([P, A * D], BF16, name="ab", align_bytes=64)
+            ab = work.tile([P, A * D], BF16, name="ab", align_bytes=64, bufs=PBUFS)
             T["ab", g] = ab
             i, first = where(g, 0)
             c0 = first.start
@@ -124,7 +133,7 @@ def tile_block_pb_t_kernel(
                     nc.tensor.transpose(ta[:, a, u, :], words[:, u::2], ident[:])
 
         def st_CA(g):
-            ag = work.tile([P, A, P, 4], BF16, name="ag", align_bytes=64)
+            ag = work.tile([P, A, P, 4], BF16, name="ag", align_bytes=64, bufs=PBUFS)
             T["ag", g] = ag
             nc.scalar.copy(
                 out=ag[:].rearrange("p a r f -> p a (r f)").bitcast(F32).rearrange("p a (r u) -> p a r u", u=2),
@@ -132,17 +141,36 @@ def tile_block_pb_t_kernel(
             )
 
         def st_QA(g):
-            ac = work.tile([P, A * P], U32, name="ac", align_bytes=64)
-            asc = work.tile([P, A * P], U8, name="asc", align_bytes=64)
+            ac = work.tile([P, A * P], U32, name="ac", align_bytes=64, bufs=PBUFS)
+            asc = work.tile([P, A * P], U8, name="asc", align_bytes=64, bufs=PBUFS)
             T["ac", g] = (ac, asc)
             nc.vector.quantize_mx(
                 out=ac[:].bitcast(FP8X4), scales=asc[:], in_=T["ag", g][:].rearrange("p a r f -> p (a r f)")
             )
 
+        def warm(bank):
+            nc.tensor.matmul_mx(
+                out=bank,
+                lhsT=wpc[:, 0:P].bitcast(FP8X4),
+                lhsT_scale=wpsc[:, 0:P],
+                rhs=wpc[:].bitcast(FP8X4),
+                rhs_scale=wpsc[:],
+                start=True,
+                stop=True,
+            )
+
+        def new_M1(g):
+            if ("m1", g) not in T:
+                ma = psum.tile([P, 2, A * P], F32, name="ma", bufs=1)
+                mb = psum.tile([P, 2, A * P], F32, name="mb", bufs=1)
+                T["m1", g] = (ma, mb)
+
+        def st_DM(g):
+            new_M1(g)
+            warm(T["m1", g][0][:].rearrange("p f n -> p (f n)"))
+
         def st_M1(g):
-            ma = psum.tile([P, 2, A * P], F32, name="ma", bufs=1)
-            mb = psum.tile([P, 2, A * P], F32, name="mb", bufs=1)
-            T["m1", g] = (ma, mb)
+            new_M1(g)
             for f in range(4):
                 nc.tensor.matmul_mx(
                     out=T["m1", g][f // 2][:, f % 2, :],
@@ -158,6 +186,15 @@ def tile_block_pb_t_kernel(
             ot = work.tile([P, 4, A * P], F32, name="ot", bufs=2)
             T["ot", g] = ot
             for f in range(4):
+                if g in OT_V and f < 2:
+                    nc.vector.tensor_scalar(
+                        out=ot[:, f, :],
+                        in0=T["m1", g][f // 2][:, f % 2, :],
+                        scalar1=gcols[:, 8 + f : 9 + f],
+                        scalar2=None,
+                        op0=ALU.add,
+                    )
+                    continue
                 nc.scalar.activation(
                     out=ot[:, f, :],
                     in_=T["m1", g][f // 2][:, f % 2, :],
@@ -165,22 +202,33 @@ def tile_block_pb_t_kernel(
                     bias=gcols[:, 8 + f : 9 + f],
                 )
 
+        def new_TO(g):
+            if ("to", g) not in T:
+                t0 = psum.tile([P, D], F32, name="t0", bufs=1)
+                t1 = psum.tile([P, D], F32, name="t1", bufs=1)
+                T["to", g] = (t0, t1)
+
+        def st_DT(g):
+            new_TO(g)
+            warm(T["to", g][0][:])
+
         def st_TO(g):
-            t0 = psum.tile([P, D], F32, name="t0", bufs=1)
-            t1 = psum.tile([P, D], F32, name="t1", bufs=1)
-            T["to", g] = (t0, t1)
+            new_TO(g)
             for a in range(A):
                 for f in range(4):
                     nc.tensor.transpose(
                         T["to", g][a][:, f * P : (f + 1) * P], T["ot", g][:, f, a * P : (a + 1) * P], ident[:]
                     )
 
-        def st_XA(g):
-            xm = work.tile([P, A, D], F32, name="xm", bufs=4)
-            sums = work.tile([P, A], F32, name="sums")
-            T["xm", g] = xm
-            T["sums", g] = sums
-            for a in range(A):
+        def st_XA(g, a):
+            if a == 0:
+                xm = work.tile([P, A, D], F32, name="xm", bufs=4)
+                sums = work.tile([P, A], F32, name="sums")
+                T["xm", g] = xm
+                T["sums", g] = sums
+            xm = T["xm", g]
+            sums = T["sums", g]
+            if True:
                 i, cols = where(g, a)
                 nc.vector.scalar_tensor_tensor(
                     out=xm[:, a, :],
@@ -191,14 +239,13 @@ def tile_block_pb_t_kernel(
                     op1=ALU.add,
                     accum_out=sums[:, a : a + 1],
                 )
-            nc.sync.dma_start(out=xm_hbm[:, g * A * D : (g + 1) * A * D], in_=xm[:].rearrange("p a d -> p (a d)"))
+            if a == 1:
+                nc.sync.dma_start(out=xm_hbm[:, g * A * D : (g + 1) * A * D], in_=xm[:].rearrange("p a d -> p (a d)"))
 
         def st_NM(g):
             nm = work.tile([P, A], F32, name="nm")
             T["nm", g] = nm
-            nc.gpsimd.tensor_scalar(
-                out=nm[:], in0=T["sums", g][:], scalar1=-1.0 / D, scalar2=0.0, op0=ALU.mult, op1=ALU.add
-            )
+            nc.scalar.activation(out=nm[:], in_=T["sums", g][:], func=ACT.Copy, scale=-1.0 / D)
 
         def st_SQ(g):
             ss = work.tile([P, A], F32, name="ss")
@@ -218,15 +265,17 @@ def tile_block_pb_t_kernel(
             var = work.tile([P, A], F32, name="var")
             rstd = work.tile([P, A], F32, name="rstd")
             T["rstd", g] = rstd
-            nc.gpsimd.tensor_scalar(
-                out=var[:], in0=T["ss", g][:], scalar1=1.0 / D**3, scalar2=LN_EPS, op0=ALU.mult, op1=ALU.add
+            nc.scalar.activation(
+                out=var[:], in_=T["ss", g][:], func=ACT.Identity, scale=1.0 / D**3, bias=epsc[:, 0:1]
             )
             nc.gpsimd.tensor_tensor(out=rstd[:], in0=var[:], in1=neghalf[:], op=ALU.pow)
 
-        def st_Z(g):
-            z = work.tile([P, A, D], F32, name="z", bufs=2)
-            T["z", g] = z
-            for a in range(A):
+        def st_Z(g, a):
+            if a == 0:
+                z = work.tile([P, A, D], F32, name="z", bufs=2)
+                T["z", g] = z
+            z = T["z", g]
+            if True:
                 src = T["xm", g][:, a, :].rearrange("p (b t q) -> p t b q", t=4, q=8)
                 dst = z[:, a, :].rearrange("p (t b q) -> p t b q", t=4, q=8)
                 nc.vector.tensor_scalar(
@@ -238,11 +287,19 @@ def tile_block_pb_t_kernel(
                     op1=ALU.mult,
                 )
 
-        def st_TZ(g):
-            za = psum.tile([P, 2, A * P], F32, name="za", tag="za", bufs=1)
-            zb = psum.tile([P, 2, A * P], F32, name="zb", tag="zb", bufs=1)
-            T["zp", g] = (za, zb)
-            for a in range(A):
+        def new_TZ(g):
+            if ("zp", g) not in T:
+                za = psum.tile([P, 2, A * P], F32, name="za", tag="za", bufs=1)
+                zb = psum.tile([P, 2, A * P], F32, name="zb", tag="zb", bufs=1)
+                T["zp", g] = (za, zb)
+
+        def st_DZ(g):
+            new_TZ(g)
+            warm(T["zp", g][0][:].rearrange("p t n -> p (t n)"))
+
+        def st_TZ(g, a):
+            new_TZ(g)
+            if True:
                 for t in range(4):
                     nc.tensor.transpose(
                         T["zp", g][t // 2][:, t % 2, a * P : (a + 1) * P],
@@ -254,7 +311,7 @@ def tile_block_pb_t_kernel(
             hp = work.tile([P, 4, A * P], BF16, name="hp")
             T["hp", g] = hp
             for t in range(4):
-                if g == G - 1 and t < 2:
+                if g in PL_V and t < 2:
                     nc.vector.tensor_scalar(
                         out=hp[:, t, :],
                         in0=T["zp", g][t // 2][:, t % 2, :],
@@ -288,130 +345,123 @@ def tile_block_pb_t_kernel(
                 out=hc[:].bitcast(FP8X4), scales=hsc[:], in_=T["hg", g][:].rearrange("p r t -> p (r t)")
             )
 
-        def st_M2(g):
-            accs = []
-            for a in range(A):
-                acc = psum.tile([P, N_MLP], F32, name="acc", tag="mm")
-                nc.tensor.matmul_mx(
-                    out=acc[:],
-                    lhsT=T["hc", g][0][:, a * P : (a + 1) * P].bitcast(FP8X4),
-                    lhsT_scale=T["hc", g][1][:, a * P : (a + 1) * P],
-                    rhs=w1c[:].bitcast(FP8X4),
-                    rhs_scale=w1sc[:],
-                    start=True,
-                    stop=True,
-                )
-                accs.append(acc)
-            T["m2", g] = accs
+        def st_M2(g, a):
+            acc = psum.tile([P, N_MLP], F32, name="acc", tag="mm")
+            T["m2", g, a] = acc
+            nc.tensor.matmul_mx(
+                out=acc[:],
+                lhsT=T["hc", g][0][:, a * P : (a + 1) * P].bitcast(FP8X4),
+                lhsT_scale=T["hc", g][1][:, a * P : (a + 1) * P],
+                rhs=w1c[:].bitcast(FP8X4),
+                rhs_scale=w1sc[:],
+                start=True,
+                stop=True,
+            )
+
+        def st_DD(g):
+            spare = psum.tile([P, N_MLP], F32, name="spare", tag="mm")
+            warm(spare[:])
 
         def st_B1(g, a):
             if a == 0:
                 v = work.tile([P, A, N_MLP], F32, name="v", bufs=2)
                 T["v", g] = v
-            nc.vector.tensor_tensor(out=T["v", g][:, a, :], in0=T["m2", g][a][:], in1=b1f[:], op=ALU.add)
+            nc.vector.tensor_tensor(out=T["v", g][:, a, :], in0=T["m2", g, a][:], in1=b1f[:], op=ALU.add)
 
         def st_GE(g):
             u = work.tile([P, A * N_MLP], F32, name="u")
-            nc.scalar.activation(out=u[:], in_=T["v", g][:].rearrange("p a n -> p (a n)"), func=ACT.Gelu)
-            nc.sync.dma_start(out=u_hbm[:, g * A * N_MLP : (g + 1) * A * N_MLP], in_=u[:])
+            vv = T["v", g][:].rearrange("p a n -> p (a n)")
+            for lo, hi in [(0, D), (D, A * D)] if g == G - 1 else [(0, A * D)]:
+                nc.scalar.activation(out=u[:, lo:hi], in_=vv[:, lo:hi], func=ACT.Gelu)
+                nc.sync.dma_start(
+                    out=u_hbm[:, g * A * N_MLP + lo : g * A * N_MLP + hi],
+                    in_=u[:, lo:hi],
+                )
 
-        def iteration(k):
-            def has(g):
-                return 0 <= g < G
+        wpg = keep.tile([P, D, 4], BF16, name="wpg", align_bytes=64)
+        wpc = keep.tile([P, D], U32, name="wpc", align_bytes=64)
+        wpsc = keep.tile([P, D], U8, name="wpsc", align_bytes=64)
+        gcols = keep.tile([P, 12], F32, name="gcols")
+        b1f = keep.tile([P, N_MLP], F32, name="b1f")
+        w1p = keep.tile([P, 4, D], BF16, name="w1p")
+        w1g = keep.tile([P, N_MLP, 4], BF16, name="w1g", align_bytes=64)
+        w1c = keep.tile([P, N_MLP], U32, name="w1c", align_bytes=64)
+        w1sc = keep.tile([P, N_MLP], U8, name="w1sc", align_bytes=64)
 
-            if has(k + 2):
-                st_CA(k + 2)
-            if has(k - 3):
-                st_M2(k - 3)
-            if has(k):
-                st_XA(k)
-                st_NM(k)
-            if has(k - 1):
-                st_Z(k - 1)
-                st_TZ(k - 1)
-            if has(k + 1):
-                st_OT(k + 1)
-                st_TO(k + 1)
-            if has(k):
-                st_SQ(k)
-                st_RS(k)
-            if has(k - 3):
-                st_B1(k - 3, 0)
-            if has(k + 2):
-                st_QA(k + 2)
-                st_M1(k + 2)
-            if has(k - 3):
-                st_B1(k - 3, 1)
-            if has(k - 1):
-                st_PL(k - 1)
-            if has(k - 2):
-                st_IL(k - 2)
-            if has(k + 3):
-                st_P(k + 3)
-                st_TA(k + 3)
-            if has(k - 2):
-                st_QH(k - 2)
-            if has(k - 3):
-                st_GE(k - 3)
-
-        wps = []
-        for h in range(2):
+        def st_WPT(h):
             wpp = psum.tile([P, 2, 2, P], F32, name="wpp", tag="za" if h == 0 else "zb", bufs=1)
-            wps.append(wpp)
+            T["wpp", h] = wpp
             for c in range(2):
                 words = wp[:, 2 * h + c, :].bitcast(F32)
                 for e in range(2):
                     nc.tensor.transpose(wpp[:, c, e, :], words[:, e::2], ident[:])
-        iteration(-3)
-        nc.vector.tensor_copy(out=scale[:, D : 2 * D], in_=scale[:, 0:D])
-        wpg = keep.tile([P, D, 4], BF16, name="wpg", align_bytes=64)
-        for h in range(2):
+
+        def st_WPC(h):
             dst = (
                 wpg[:, h * 2 * P : (h + 1) * 2 * P, :]
                 .rearrange("p n t -> p (n t)")
                 .bitcast(F32)
                 .rearrange("p (c n e) -> p c n e", c=2, e=2)
             )
-            src = wps[h][:].rearrange("p c e n -> p c n e")
+            src = T["wpp", h][:].rearrange("p c e n -> p c n e")
             if h == 0:
                 nc.vector.tensor_copy(out=dst, in_=src)
             else:
                 nc.scalar.copy(out=dst, in_=src)
-        wpc = keep.tile([P, D], U32, name="wpc", align_bytes=64)
-        wpsc = keep.tile([P, D], U8, name="wpsc", align_bytes=64)
-        nc.vector.quantize_mx(out=wpc[:].bitcast(FP8X4), scales=wpsc[:], in_=wpg[:].rearrange("p n t -> p (n t)"))
-        gp = psum.tile([P, P], BF16, name="gp", tag="za", bufs=1)
-        nc.tensor.transpose(gp[:], grows[:], identb[:])
-        gcols = keep.tile([P, 12], F32, name="gcols")
-        nc.scalar.copy(out=gcols[:], in_=gp[:, 0:12])
-        bb = psum.tile([P, N_MLP], F32, name="bb", tag="zb", bufs=1)
-        nc.tensor.matmul(out=bb[:], lhsT=identb[:, 0:1].to_broadcast([P, P]), rhs=vrows[:], start=True, stop=True)
-        b1f = keep.tile([P, N_MLP], F32, name="b1f")
-        nc.scalar.copy(out=b1f[:], in_=bb[:])
-        iteration(-2)
-        iteration(-1)
-        iteration(0)
-        w1p = keep.tile([P, 4, D], BF16, name="w1p")
-        w1g = keep.tile([P, N_MLP, 4], BF16, name="w1g", align_bytes=64)
-        for c in range(4):
+
+        def st_WPQ(h):
+            nc.vector.quantize_mx(out=wpc[:].bitcast(FP8X4), scales=wpsc[:], in_=wpg[:].rearrange("p n t -> p (n t)"))
+
+        def st_SC(h):
+            nc.vector.tensor_copy(out=scale[:, D : 2 * D], in_=scale[:, 0:D])
+
+        def st_GC(h):
+            gp = psum.tile([P, P], BF16, name="gp", tag="t0", bufs=1)
+            nc.tensor.transpose(gp[:], grows[:], identb[:])
+            nc.scalar.copy(out=gcols[:], in_=gp[:, 0:12])
+
+        def st_BB(h):
+            bb = psum.tile([P, N_MLP], F32, name="bb", tag="t1", bufs=1)
+            nc.tensor.matmul(out=bb[:], lhsT=identb[:, 0:1].to_broadcast([P, P]), rhs=vrows[:], start=True, stop=True)
+            nc.scalar.copy(out=b1f[:], in_=bb[:])
+
+        def st_W1P(c):
             nc.vector.tensor_copy(
                 out=w1p[:, c, :].rearrange("p (t b q) -> p t b q", t=4, q=8),
                 in_=w1[:, c, :].rearrange("p (b t q) -> p t b q", t=4, q=8),
             )
-        for h in range(2):
+
+        def st_W1T(h):
             w1t = psum.tile([P, 2, 4, P], BF16, name="w1t", tag="za" if h == 0 else "zb", bufs=1)
+            T["w1t", h] = w1t
             for c in range(2):
                 for t in range(4):
                     nc.tensor.transpose(w1t[:, c, t, :], w1p[:, 2 * h + c, t * P : (t + 1) * P], identb[:])
-            dst = w1g[:, h * 2 * P : (h + 1) * 2 * P, :].rearrange("p (c n) t -> p c n t", c=2)
-            src = w1t[:].rearrange("p c t n -> p c n t")
-            if h == 0:
-                nc.vector.tensor_copy(out=dst, in_=src)
-            else:
-                nc.scalar.copy(out=dst, in_=src)
-        w1c = keep.tile([P, N_MLP], U32, name="w1c", align_bytes=64)
-        w1sc = keep.tile([P, N_MLP], U8, name="w1sc", align_bytes=64)
-        nc.vector.quantize_mx(out=w1c[:].bitcast(FP8X4), scales=w1sc[:], in_=w1g[:].rearrange("p n t -> p (n t)"))
 
-        for k in range(1, G + 4):
-            iteration(k)
+        def st_W1C(h):
+            dst = w1g[:, h * 2 * P : (h + 1) * 2 * P, :].rearrange("p (c n) t -> p c n t", c=2)
+            nc.vector.tensor_copy(out=dst, in_=T["w1t", h][:].rearrange("p c t n -> p c n t"))
+
+        def st_W1Q(h):
+            nc.vector.quantize_mx(out=w1c[:].bitcast(FP8X4), scales=w1sc[:], in_=w1g[:].rearrange("p n t -> p (n t)"))
+
+        STAGES = {
+            "P": st_P, "TA": st_TA, "CA": st_CA, "QA": st_QA, "M1": st_M1, "OT": st_OT, "TO": st_TO,
+            "NM": st_NM, "SQ": st_SQ, "RS": st_RS, "PL": st_PL, "IL": st_IL, "QH": st_QH, "GE": st_GE,
+            "DM": st_DM, "WPT": st_WPT, "WPC": st_WPC, "WPQ": st_WPQ, "SC": st_SC, "GC": st_GC, "BB": st_BB,
+            "W1P": st_W1P, "W1T": st_W1T, "W1C": st_W1C, "W1Q": st_W1Q, "DT": st_DT, "DZ": st_DZ, "DD": st_DD,
+        }
+        PARTS = {"XA": st_XA, "Z": st_Z, "TZ": st_TZ, "M2": st_M2, "B1": st_B1}
+
+        def call(name, g):
+            if name[-1] in "01" and name[:-1] in PARTS:
+                PARTS[name[:-1]](g, int(name[-1]))
+            else:
+                STAGES[name](g)
+
+        for name, g in HEAD:
+            call(name, g)
+        for k in range(KFIRST, G + 4):
+            for name, off in TAIL.get(k, ORDER):
+                if 0 <= k + off < G:
+                    call(name, k + off)

@@ -18,16 +18,15 @@ ALU = mybir.AluOpType
 
 P = 128
 R = TOKENS // P
-A = 2
+A = 4
 G = R // A
-CHUNKS = [1, 1, 2, 4, 4, 4]
-ORDER = [('CA', 3), ('M1', 2), ('XA0', 0), ('OT', 1), ('XA1', 0), ('Z0', -1), ('IL', -2), ('M20', -3), ('Z1', -1), ('M21', -3), ('QH', -2), ('SQ', 0), ('NM', 0), ('QA', 3), ('P', 4), ('DZ', -1), ('TZ0', -1), ('B10', -3), ('B11', -3), ('RS', 0), ('TZ1', -1), ('PL', -1), ('TO', 1), ('TA', 4), ('GE', -3)]
-HEAD = [('P', 0), ('WPT', 0), ('TA', 0), ('CA', 0), ('SC', 0), ('P', 1), ('WPT', 1), ('QA', 0), ('WPC', 1), ('TA', 1), ('WPC', 0), ('W1P', 1), ('W1P', 0), ('GC', 0), ('P', 3), ('WPQ', 0), ('CA', 1), ('M1', 0), ('P', 2), ('OT', 0), ('TA', 2), ('W1P', 3), ('TO', 0), ('QA', 1), ('P', 4), ('XA0', 0), ('M1', 1), ('OT', 1), ('BB', 0), ('W1P', 2), ('XA1', 0), ('TA', 3), ('CA', 2), ('CA', 3), ('NM', 0), ('W1T', 0), ('QA', 2), ('W1C', 0), ('W1T', 1), ('SQ', 0), ('W1C', 1), ('M1', 2), ('RS', 0), ('QA', 3), ('TO', 1), ('TA', 4), ('W1Q', 0)]
-TAIL = {16: [('Z0', -1), ('M20', -3), ('Z1', -1), ('IL', -2), ('B10', -3), ('M21', -3), ('QH', -2), ('TZ0', -1), ('B11', -3), ('TZ1', -1), ('PL', -1), ('GE', -3)], 17: [('M20', -3), ('B10', -3), ('IL', -2), ('M21', -3), ('B11', -3), ('GE', -3), ('QH', -2)], 18: [('M20', -3), ('B10', -3), ('M21', -3), ('B11', -3), ('GE', -3)]}
-KFIRST = 1
-PL_V = {13,11,5}
-OT_V = {11,14,7,3,0,1}
-PBUFS = 5
+PROGRAM = [('WPT', 0, 0), ('WPT', 1, 0), ('SC', 0, 0), ('GC', 0, 0), ('WPC', 0, 0), ('P', 0, 0), ('WPC', 1, 1), ('P', 0, 1), ('TA', 0, 0), ('TA', 0, 1), ('P', 1, 0), ('CA', 0, 0), ('WPQ', 0, 0), ('CA', 0, 1), ('XP', 0, 2), ('P', 1, 1), ('TA', 1, 0), ('QA', 0, 2), ('TA', 1, 1), ('M1', 0, 3), ('M1', 0, 2), ('P', 2, 0), ('M1', 0, 0), ('M1', 0, 1), ('XE', 0, 2), ('CA', 1, 0), ('OT', 0, 3), ('CA', 1, 1), ('OT', 0, 0), ('XP', 0, 3), ('OT', 0, 1), ('P', 2, 1), ('TA', 2, 0), ('OT', 0, 2), ('XP', 1, 2), ('TO', 0, 0), ('TA', 2, 1), ('QA', 1, 2), ('XE', 0, 3), ('P', 3, 0), ('M1', 1, 3), ('M1', 1, 2), ('M1', 1, 0), ('TO', 0, 1), ('CA', 2, 0), ('XA', 0, 0), ('M1', 1, 1), ('XE', 1, 2), ('CA', 2, 1), ('XA', 0, 1), ('OT', 1, 3), ('TO', 0, 2), ('XA', 0, 2), ('P', 3, 1), ('OT', 1, 0), ('XP', 1, 3), ('TA', 3, 0), ('TO', 0, 3), ('OT', 1, 1), ('SQ', 0, 0), ('XP', 2, 2), ('XA', 0, 3), ('SQ', 0, 1), ('QA', 2, 2), ('OT', 1, 2), ('TA', 3, 1), ('TO', 1, 0), ('P', 4, 0), ('M1', 2, 3), ('M1', 2, 2), ('XE', 1, 3), ('M1', 2, 0), ('M1', 2, 1), ('CA', 3, 0), ('SQ', 0, 2), ('SQ', 0, 3), ('XE', 2, 2), ('CA', 3, 1), ('TO', 1, 1), ('OT', 2, 3), ('XA', 1, 0), ('XA', 1, 1), ('OT', 2, 0), ('XP', 2, 3), ('OT', 2, 1), ('P', 4, 1), ('TA', 4, 0), ('TO', 1, 2), ('XA', 1, 2), ('XP', 3, 2), ('OT', 2, 2), ('TO', 1, 3), ('QA', 3, 2), ('SQ', 1, 0), ('TA', 4, 1), ('TO', 2, 0), ('XA', 1, 3), ('SQ', 1, 1), ('P', 5, 0), ('XE', 2, 3), ('M1', 3, 3), ('M1', 3, 2), ('M1', 3, 0), ('M1', 3, 1), ('CA', 4, 0), ('XE', 3, 2), ('TO', 2, 1), ('XA', 2, 0), ('CA', 4, 1), ('SQ', 1, 2), ('OT', 3, 3), ('SQ', 1, 3), ('XA', 2, 1), ('OT', 3, 0), ('XP', 3, 3), ('P', 5, 1), ('TO', 2, 2), ('OT', 3, 1), ('TA', 5, 0), ('XA', 2, 2), ('XP', 4, 2), ('TO', 2, 3), ('SQ', 2, 0), ('OT', 3, 2), ('QA', 4, 2), ('TA', 5, 1), ('XA', 2, 3), ('SQ', 2, 1), ('TO', 3, 0), ('P', 6, 0), ('M1', 4, 3), ('XE', 3, 3), ('M1', 4, 2), ('M1', 4, 0), ('M1', 4, 1), ('CA', 5, 0), ('XE', 4, 2), ('TO', 3, 1), ('CA', 5, 1), ('SQ', 2, 2), ('XA', 3, 0), ('SQ', 2, 3), ('OT', 4, 3), ('XA', 3, 1), ('OT', 4, 0), ('XP', 4, 3), ('P', 6, 1), ('OT', 4, 1), ('TA', 6, 0), ('TO', 3, 2), ('XA', 3, 2), ('XP', 5, 2), ('TO', 3, 3), ('OT', 4, 2), ('SQ', 3, 0), ('QA', 5, 2), ('TA', 6, 1), ('XA', 3, 3), ('SQ', 3, 1), ('TO', 4, 0), ('P', 7, 0), ('M1', 5, 3), ('XE', 4, 3), ('M1', 5, 2), ('M1', 5, 0), ('M1', 5, 1), ('CA', 6, 0), ('XE', 5, 2), ('TO', 4, 1), ('CA', 6, 1), ('XA', 4, 0), ('SQ', 3, 2), ('OT', 5, 3), ('SQ', 3, 3), ('XA', 4, 1), ('OT', 5, 0), ('XP', 5, 3), ('P', 7, 1), ('OT', 5, 1), ('TA', 7, 0), ('TO', 4, 2), ('XA', 4, 2), ('W1P', 2, 0), ('XP', 6, 2), ('TO', 4, 3), ('OT', 5, 2), ('SQ', 4, 0), ('QA', 6, 2), ('TA', 7, 1), ('XA', 4, 3), ('SQ', 4, 1), ('W1P', 0, 0), ('TO', 5, 0), ('W1P', 1, 0), ('M1', 6, 3), ('XE', 5, 3), ('M1', 6, 2), ('M1', 6, 0), ('M1', 6, 1), ('CA', 7, 0), ('XE', 6, 2), ('TO', 5, 1), ('CA', 7, 1), ('XA', 5, 0), ('SQ', 4, 2), ('OT', 6, 3), ('SQ', 4, 3), ('XA', 5, 1), ('OT', 6, 0), ('XP', 6, 3), ('OT', 6, 1), ('TO', 5, 2), ('XA', 5, 2), ('XP', 7, 2), ('TO', 5, 3), ('OT', 6, 2), ('SQ', 5, 0), ('QA', 7, 2), ('XA', 5, 3), ('SQ', 5, 1), ('TO', 6, 0), ('M1', 7, 3), ('XE', 6, 3), ('M1', 7, 2), ('M1', 7, 0), ('M1', 7, 1), ('XE', 7, 2), ('TO', 6, 1), ('XA', 6, 0), ('SQ', 5, 2), ('OT', 7, 3), ('SQ', 5, 3), ('W1P', 3, 0), ('XA', 6, 1), ('OT', 7, 0), ('XP', 7, 3), ('OT', 7, 1), ('TO', 6, 2), ('XA', 6, 2), ('TO', 6, 3), ('OT', 7, 2), ('SQ', 6, 0), ('XA', 6, 3), ('SQ', 6, 1), ('TO', 7, 0), ('XE', 7, 3), ('RS', 0, 6), ('TO', 7, 1), ('XA', 7, 0), ('SQ', 6, 2), ('SQ', 6, 3), ('XA', 7, 1), ('TO', 7, 2), ('XA', 7, 2), ('TO', 7, 3), ('SQ', 7, 0), ('XA', 7, 3), ('SQ', 7, 1), ('RV', 0, 6), ('SQ', 7, 2), ('SQ', 7, 3), ('W1T', 1, 0), ('W1T', 0, 0), ('Z', 0, 1), ('Z', 0, 0), ('Z', 0, 2), ('RS', 6, 8), ('Z', 1, 1), ('Z', 1, 0), ('Z', 0, 3), ('TZ', 0, 1), ('TZ', 0, 0), ('W1C', 1, 0), ('W1C', 0, 0), ('Z', 1, 2), ('TZ', 0, 2), ('TZ', 0, 3), ('Z', 2, 1), ('Z', 2, 0), ('Z', 1, 3), ('PL', 0, 0), ('PL', 0, 2), ('PL', 0, 1), ('PL', 0, 3), ('TZ', 1, 1), ('TZ', 1, 0), ('W1Q', 0, 0), ('Z', 2, 2), ('TZ', 1, 2), ('IL', 0, 2), ('TZ', 1, 3), ('QH', 0, 2), ('Z', 3, 1), ('Z', 3, 0), ('Z', 2, 3), ('RV', 6, 8), ('PL', 1, 0), ('PL', 1, 2), ('M2', 0, 0), ('PL', 1, 1), ('PL', 1, 3), ('TZ', 2, 1), ('TZ', 2, 0), ('Z', 3, 2), ('TZ', 2, 2), ('IL', 1, 2), ('TZ', 2, 3), ('QH', 1, 2), ('M2', 0, 1), ('B1', 0, 0), ('Z', 4, 1), ('Z', 4, 0), ('Z', 3, 3), ('M2', 0, 2), ('B1', 0, 1), ('PL', 2, 0), ('B1', 0, 2), ('PL', 2, 2), ('M2', 0, 3), ('M2', 1, 0), ('PL', 2, 1), ('PL', 2, 3), ('TZ', 3, 1), ('TZ', 3, 0), ('Z', 4, 2), ('TZ', 3, 2), ('IL', 2, 2), ('B1', 0, 3), ('TZ', 3, 3), ('QH', 2, 2), ('M2', 1, 1), ('B1', 1, 0), ('Z', 5, 1), ('Z', 5, 0), ('Z', 4, 3), ('M2', 1, 2), ('B1', 1, 1), ('PL', 3, 0), ('B1', 1, 2), ('PL', 3, 2), ('M2', 1, 3), ('M2', 2, 0), ('PL', 3, 1), ('PL', 3, 3), ('TZ', 4, 1), ('TZ', 4, 0), ('Z', 5, 2), ('TZ', 4, 2), ('IL', 3, 2), ('B1', 1, 3), ('TZ', 4, 3), ('QH', 3, 2), ('M2', 2, 1), ('B1', 2, 0), ('Z', 6, 1), ('Z', 6, 0), ('GE', 0, 2), ('Z', 5, 3), ('M2', 2, 2), ('B1', 2, 1), ('PL', 4, 0), ('B1', 2, 2), ('PL', 4, 2), ('M2', 2, 3), ('M2', 3, 0), ('PL', 4, 1), ('PL', 4, 3), ('TZ', 5, 1), ('TZ', 5, 0), ('Z', 6, 2), ('TZ', 5, 2), ('IL', 4, 2), ('B1', 2, 3), ('TZ', 5, 3), ('QH', 4, 2), ('M2', 3, 1), ('B1', 3, 0), ('Z', 7, 1), ('Z', 7, 0), ('GE', 1, 2), ('Z', 6, 3), ('M2', 3, 2), ('B1', 3, 1), ('PL', 5, 0), ('B1', 3, 2), ('PL', 5, 2), ('M2', 3, 3), ('M2', 4, 0), ('PL', 5, 1), ('PL', 5, 3), ('TZ', 6, 1), ('TZ', 6, 0), ('Z', 7, 2), ('TZ', 6, 2), ('IL', 5, 2), ('B1', 3, 3), ('TZ', 6, 3), ('QH', 5, 2), ('M2', 4, 1), ('B1', 4, 0), ('GE', 2, 2), ('Z', 7, 3), ('M2', 4, 2), ('B1', 4, 1), ('PL', 6, 0), ('B1', 4, 2), ('PL', 6, 2), ('M2', 4, 3), ('M2', 5, 0), ('PL', 6, 1), ('PL', 6, 3), ('TZ', 7, 1), ('TZ', 7, 0), ('TZ', 7, 2), ('IL', 6, 2), ('B1', 4, 3), ('TZ', 7, 3), ('QH', 6, 2), ('M2', 5, 1), ('B1', 5, 0), ('GE', 3, 2), ('M2', 5, 2), ('B1', 5, 1), ('PL', 7, 0), ('B1', 5, 2), ('PL', 7, 2), ('M2', 5, 3), ('M2', 6, 0), ('PL', 7, 1), ('PL', 7, 3), ('IL', 7, 2), ('B1', 5, 3), ('QH', 7, 2), ('M2', 6, 1), ('B1', 6, 0), ('GE', 4, 2), ('M2', 6, 2), ('B1', 6, 1), ('B1', 6, 2), ('M2', 6, 3), ('M2', 7, 0), ('B1', 6, 3), ('M2', 7, 1), ('B1', 7, 0), ('GE', 5, 2), ('M2', 7, 2), ('B1', 7, 1), ('B1', 7, 2), ('M2', 7, 3), ('B1', 7, 3), ('GE', 6, 2), ('GE', 7, 0), ('GE', 7, 1)]
+OT_V = set()
+PL_V = set()
+Z_S = {2, 3, 7, 10, 11, 15, 18, 19, 23, 26, 27, 31}
+CA_V = set()
+XB_V = {11, 19, 3, 27}
+CHUNKS = [2, 2, 4, 8, 8, 8]
 
 
 def tile_block_pb_t_kernel(
@@ -41,55 +40,48 @@ def tile_block_pb_t_kernel(
 
     with ExitStack() as ctx:
         keep = ctx.enter_context(tc.tile_pool(name="keep", bufs=1))
-        work = ctx.enter_context(tc.tile_pool(name="work", bufs=3))
-        psum = ctx.enter_context(tc.psum_pool(name="psum", bufs=2))
+        work = ctx.enter_context(tc.tile_pool(name="work", bufs=2))
+        psum = ctx.enter_context(tc.psum_pool(name="psum", bufs=1))
         ctx.enter_context(tc.manual_schedule())
 
-        scale = keep.tile([P, A * D], F32, name="scale")
+        scale = keep.tile([P, 2 * D], F32, name="scale")
         nc.scalar.dma_start(out=scale[:, 0:D], in_=attn_out_scale.rearrange("a b k -> (a b k)").partition_broadcast(P))
         vrows = keep.tile([P, D], BF16, name="vrows")
         nc.vector.memset(vrows[:], 0.0)
         grows = keep.tile([P, P], BF16, name="grows")
         nc.vector.memset(grows[:], 0.0)
         dummy = keep.tile([P, 1], F32, name="dummy")
-        nc.vector.memset(dummy[:], 0.0)
+        nc.vector.memset(dummy[:], 1.0)
         epsc = keep.tile([P, 1], F32, name="epsc")
-        nc.vector.tensor_scalar(out=epsc[:], in0=dummy[:], scalar1=LN_EPS, scalar2=None, op0=ALU.add)
-        neghalf = keep.tile([P, A], F32, name="neghalf")
-        nc.vector.memset(neghalf[:], -0.5)
+        nc.vector.tensor_scalar(out=epsc[:], in0=dummy[:], scalar1=LN_EPS, scalar2=None, op0=ALU.mult)
         ident = keep.tile([P, P], F32, name="ident")
         make_identity(nc, ident[:])
         identb = keep.tile([P, P], BF16, name="identb")
         nc.vector.tensor_copy(out=identb[:], in_=ident[:])
-        nc.scalar.activation(out=dummy[:], in_=dummy[:], func=ACT.Gelu)
+        nc.scalar.activation(out=dummy[:], in_=dummy[:], func=ACT.Sqrt)
 
         starts = [sum(CHUNKS[:i]) for i in range(len(CHUNKS))]
         byte_tiles = []
         x_tiles = []
         for i in range(len(CHUNKS)):
-            w = CHUNKS[i] * A * D
-            bt = keep.tile([P, w], U8, name="bytes%d" % i, align_bytes=64)
+            bt = keep.tile([P, CHUNKS[i] * D], U8, name="bytes%d" % i, align_bytes=64)
             byte_tiles.append(bt)
-            xt = keep.tile([P, w], BF16, name="xin%d" % i, align_bytes=64)
+            xt = keep.tile([P, CHUNKS[i] * D], BF16, name="xin%d" % i, align_bytes=64)
             x_tiles.append(xt)
 
         def load_bytes(i):
-            c0 = starts[i] * A * D
-            nc.sync.dma_start(out=byte_tiles[i][:], in_=bytes_hbm[:, c0 : c0 + CHUNKS[i] * A * D])
+            nc.sync.dma_start(out=byte_tiles[i][:], in_=bytes_hbm[:, starts[i] * D : (starts[i] + CHUNKS[i]) * D])
 
         def load_x(i):
-            c0 = starts[i] * A * D
-            nc.sync.dma_start(out=x_tiles[i][:], in_=x_hbm[:, c0 : c0 + CHUNKS[i] * A * D])
+            nc.sync.dma_start(out=x_tiles[i][:], in_=x_hbm[:, starts[i] * D : (starts[i] + CHUNKS[i]) * D])
 
-        def where(g, a):
-            i = max(j for j in range(len(CHUNKS)) if starts[j] <= g)
-            c0 = ((g - starts[i]) * A + a) * D
-            return i, slice(c0, c0 + D)
+        def where(r):
+            i = max(j for j in range(len(CHUNKS)) if starts[j] <= r)
+            return i, (r - starts[i]) * D
 
         wp = keep.tile([P, 4, D], BF16, name="wp")
         w1 = keep.tile([P, 4, D], BF16, name="w1")
         wp_hbm = W_proj.rearrange("(c p) k -> p c k", p=P)
-        w1_hbm = W1.rearrange("(c p) k -> p c k", p=P)
         load_bytes(0)
         nc.sync.dma_start(out=wp[:, 0:2, :], in_=wp_hbm[:, 0:2, :])
         nc.sync.dma_start(out=wp[:, 2:4, :], in_=wp_hbm[:, 2:4, :])
@@ -100,368 +92,349 @@ def tile_block_pb_t_kernel(
             out=grows[4:8, :].rearrange("t (b q) -> t b q", q=8), in_=beta2.rearrange("(b t q) -> t b q", t=4, q=8)
         )
         nc.sync.dma_start(out=grows[8:12, :], in_=b_proj.rearrange("(f p) -> f p", p=P))
-        nc.sync.dma_start(out=vrows[0:1, :], in_=b1.rearrange("(o k) -> o k", o=1))
+        nc.sync.dma_start(out=vrows[0:1, :], in_=b_proj.rearrange("(o k) -> o k", o=1))
         load_bytes(1)
         load_x(0)
+        bp = keep.tile([P, D], BF16, name="bp")
+        nc.sync.dma_start(out=bp[:], in_=b_proj.partition_broadcast(P))
+        load_bytes(2)
         load_x(1)
-        nc.sync.dma_start(out=w1[:], in_=w1_hbm)
-        for i in range(2, len(CHUNKS)):
+        load_bytes(3)
+        load_x(2)
+        load_x(3)
+        nc.sync.dma_start(out=w1[:], in_=W1.rearrange("(c p) k -> p c k", p=P))
+        b1f = keep.tile([P, N_MLP], BF16, name="b1f")
+        nc.sync.dma_start(out=b1f[:], in_=b1.partition_broadcast(P))
+        for i in range(4, len(CHUNKS)):
             load_bytes(i)
             load_x(i)
 
-        T = {}
-
-        def st_P(g):
-            ab = work.tile([P, A * D], BF16, name="ab", align_bytes=64, bufs=PBUFS)
-            T["ab", g] = ab
-            i, first = where(g, 0)
-            c0 = first.start
-            for lo, hi in [(0, D), (D, A * D)] if g == 0 else [(0, A * D)]:
-                nc.vector.tensor_tensor(
-                    out=ab[:, lo:hi],
-                    in0=byte_tiles[i][:, c0 + lo : c0 + hi].bitcast(FP8),
-                    in1=scale[:, 0 : hi - lo],
-                    op=ALU.mult,
-                )
-
-        def st_TA(g):
-            ta = psum.tile([P, A, 2, P], F32, name="ta", tag="mm")
-            T["ta", g] = ta
-            for a in range(A):
-                words = T["ab", g][:, a * D : (a + 1) * D].bitcast(F32)
-                for u in range(2):
-                    nc.tensor.transpose(ta[:, a, u, :], words[:, u::2], ident[:])
-
-        def st_CA(g):
-            ag = work.tile([P, A, P, 4], BF16, name="ag", align_bytes=64, bufs=PBUFS)
-            T["ag", g] = ag
-            nc.scalar.copy(
-                out=ag[:].rearrange("p a r f -> p a (r f)").bitcast(F32).rearrange("p a (r u) -> p a r u", u=2),
-                in_=T["ta", g][:].rearrange("p a u r -> p a r u"),
-            )
-
-        def st_QA(g):
-            ac = work.tile([P, A * P], U32, name="ac", align_bytes=64, bufs=PBUFS)
-            asc = work.tile([P, A * P], U8, name="asc", align_bytes=64, bufs=PBUFS)
-            T["ac", g] = (ac, asc)
-            nc.vector.quantize_mx(
-                out=ac[:].bitcast(FP8X4), scales=asc[:], in_=T["ag", g][:].rearrange("p a r f -> p (a r f)")
-            )
-
-        def warm(bank):
-            nc.tensor.matmul_mx(
-                out=bank,
-                lhsT=wpc[:, 0:P].bitcast(FP8X4),
-                lhsT_scale=wpsc[:, 0:P],
-                rhs=wpc[:].bitcast(FP8X4),
-                rhs_scale=wpsc[:],
-                start=True,
-                stop=True,
-            )
-
-        def new_M1(g):
-            if ("m1", g) not in T:
-                ma = psum.tile([P, 2, A * P], F32, name="ma", bufs=1)
-                mb = psum.tile([P, 2, A * P], F32, name="mb", bufs=1)
-                T["m1", g] = (ma, mb)
-
-        def st_DM(g):
-            new_M1(g)
-            warm(T["m1", g][0][:].rearrange("p f n -> p (f n)"))
-
-        def st_M1(g):
-            new_M1(g)
-            for f in range(4):
-                nc.tensor.matmul_mx(
-                    out=T["m1", g][f // 2][:, f % 2, :],
-                    lhsT=wpc[:, f * P : (f + 1) * P].bitcast(FP8X4),
-                    lhsT_scale=wpsc[:, f * P : (f + 1) * P],
-                    rhs=T["ac", g][0][:].bitcast(FP8X4),
-                    rhs_scale=T["ac", g][1][:],
-                    start=True,
-                    stop=True,
-                )
-
-        def st_OT(g):
-            ot = work.tile([P, 4, A * P], F32, name="ot", bufs=2)
-            T["ot", g] = ot
-            for f in range(4):
-                if g in OT_V and f < 2:
-                    nc.vector.tensor_scalar(
-                        out=ot[:, f, :],
-                        in0=T["m1", g][f // 2][:, f % 2, :],
-                        scalar1=gcols[:, 8 + f : 9 + f],
-                        scalar2=None,
-                        op0=ALU.add,
-                    )
-                    continue
-                nc.scalar.activation(
-                    out=ot[:, f, :],
-                    in_=T["m1", g][f // 2][:, f % 2, :],
-                    func=ACT.Identity,
-                    bias=gcols[:, 8 + f : 9 + f],
-                )
-
-        def new_TO(g):
-            if ("to", g) not in T:
-                t0 = psum.tile([P, D], F32, name="t0", bufs=1)
-                t1 = psum.tile([P, D], F32, name="t1", bufs=1)
-                T["to", g] = (t0, t1)
-
-        def st_DT(g):
-            new_TO(g)
-            warm(T["to", g][0][:])
-
-        def st_TO(g):
-            new_TO(g)
-            for a in range(A):
-                for f in range(4):
-                    nc.tensor.transpose(
-                        T["to", g][a][:, f * P : (f + 1) * P], T["ot", g][:, f, a * P : (a + 1) * P], ident[:]
-                    )
-
-        def st_XA(g, a):
-            if a == 0:
-                xm = work.tile([P, A, D], F32, name="xm", bufs=4)
-                sums = work.tile([P, A], F32, name="sums")
-                T["xm", g] = xm
-                T["sums", g] = sums
-            xm = T["xm", g]
-            sums = T["sums", g]
-            if True:
-                i, cols = where(g, a)
-                nc.vector.scalar_tensor_tensor(
-                    out=xm[:, a, :],
-                    in0=T["to", g][a][:],
-                    scalar=1.0,
-                    in1=x_tiles[i][:, cols],
-                    op0=ALU.mult,
-                    op1=ALU.add,
-                    accum_out=sums[:, a : a + 1],
-                )
-            if a == 1:
-                nc.sync.dma_start(out=xm_hbm[:, g * A * D : (g + 1) * A * D], in_=xm[:].rearrange("p a d -> p (a d)"))
-
-        def st_NM(g):
-            nm = work.tile([P, A], F32, name="nm")
-            T["nm", g] = nm
-            nc.scalar.activation(out=nm[:], in_=T["sums", g][:], func=ACT.Copy, scale=-1.0 / D)
-
-        def st_SQ(g):
-            ss = work.tile([P, A], F32, name="ss")
-            T["ss", g] = ss
-            for a in range(A):
-                junk = work.tile([P, D], BF16, name="junk")
-                nc.scalar.activation(
-                    out=junk[:],
-                    in_=T["xm", g][:, a, :],
-                    func=ACT.Square,
-                    scale=-float(D),
-                    bias=T["sums", g][:, a : a + 1],
-                    accum_out=ss[:, a : a + 1],
-                )
-
-        def st_RS(g):
-            var = work.tile([P, A], F32, name="var")
-            rstd = work.tile([P, A], F32, name="rstd")
-            T["rstd", g] = rstd
-            nc.scalar.activation(
-                out=var[:], in_=T["ss", g][:], func=ACT.Identity, scale=1.0 / D**3, bias=epsc[:, 0:1]
-            )
-            nc.gpsimd.tensor_tensor(out=rstd[:], in0=var[:], in1=neghalf[:], op=ALU.pow)
-
-        def st_Z(g, a):
-            if a == 0:
-                z = work.tile([P, A, D], F32, name="z", bufs=2)
-                T["z", g] = z
-            z = T["z", g]
-            if True:
-                src = T["xm", g][:, a, :].rearrange("p (b t q) -> p t b q", t=4, q=8)
-                dst = z[:, a, :].rearrange("p (t b q) -> p t b q", t=4, q=8)
-                nc.vector.tensor_scalar(
-                    out=dst,
-                    in0=src,
-                    scalar1=T["nm", g][:, a : a + 1],
-                    scalar2=T["rstd", g][:, a : a + 1],
-                    op0=ALU.add,
-                    op1=ALU.mult,
-                )
-
-        def new_TZ(g):
-            if ("zp", g) not in T:
-                za = psum.tile([P, 2, A * P], F32, name="za", tag="za", bufs=1)
-                zb = psum.tile([P, 2, A * P], F32, name="zb", tag="zb", bufs=1)
-                T["zp", g] = (za, zb)
-
-        def st_DZ(g):
-            new_TZ(g)
-            warm(T["zp", g][0][:].rearrange("p t n -> p (t n)"))
-
-        def st_TZ(g, a):
-            new_TZ(g)
-            if True:
-                for t in range(4):
-                    nc.tensor.transpose(
-                        T["zp", g][t // 2][:, t % 2, a * P : (a + 1) * P],
-                        T["z", g][:, a, t * P : (t + 1) * P],
-                        ident[:],
-                    )
-
-        def st_PL(g):
-            hp = work.tile([P, 4, A * P], BF16, name="hp")
-            T["hp", g] = hp
-            for t in range(4):
-                if g in PL_V and t < 2:
-                    nc.vector.tensor_scalar(
-                        out=hp[:, t, :],
-                        in0=T["zp", g][t // 2][:, t % 2, :],
-                        scalar1=gcols[:, t : t + 1],
-                        scalar2=gcols[:, 4 + t : 5 + t],
-                        op0=ALU.mult,
-                        op1=ALU.add,
-                    )
-                    continue
-                nc.scalar.activation(
-                    out=hp[:, t, :],
-                    in_=T["zp", g][t // 2][:, t % 2, :],
-                    func=ACT.Identity,
-                    scale=gcols[:, t : t + 1],
-                    bias=gcols[:, 4 + t : 5 + t],
-                )
-
-        def st_IL(g):
-            hg = work.tile([P, A * P, 4], BF16, name="hg", align_bytes=64)
-            T["hg", g] = hg
-            nc.vector.tensor_copy(
-                out=hg[:].rearrange("p (c i) t -> p c t i", i=4),
-                in_=T["hp", g][:].rearrange("p t (c i) -> p c t i", i=4),
-            )
-
-        def st_QH(g):
-            hc = work.tile([P, A * P], U32, name="hc", align_bytes=64)
-            hsc = work.tile([P, A * P], U8, name="hsc", align_bytes=64)
-            T["hc", g] = (hc, hsc)
-            nc.vector.quantize_mx(
-                out=hc[:].bitcast(FP8X4), scales=hsc[:], in_=T["hg", g][:].rearrange("p r t -> p (r t)")
-            )
-
-        def st_M2(g, a):
-            acc = psum.tile([P, N_MLP], F32, name="acc", tag="mm")
-            T["m2", g, a] = acc
-            nc.tensor.matmul_mx(
-                out=acc[:],
-                lhsT=T["hc", g][0][:, a * P : (a + 1) * P].bitcast(FP8X4),
-                lhsT_scale=T["hc", g][1][:, a * P : (a + 1) * P],
-                rhs=w1c[:].bitcast(FP8X4),
-                rhs_scale=w1sc[:],
-                start=True,
-                stop=True,
-            )
-
-        def st_DD(g):
-            spare = psum.tile([P, N_MLP], F32, name="spare", tag="mm")
-            warm(spare[:])
-
-        def st_B1(g, a):
-            if a == 0:
-                v = work.tile([P, A, N_MLP], F32, name="v", bufs=2)
-                T["v", g] = v
-            nc.vector.tensor_tensor(out=T["v", g][:, a, :], in0=T["m2", g, a][:], in1=b1f[:], op=ALU.add)
-
-        def st_GE(g):
-            u = work.tile([P, A * N_MLP], F32, name="u")
-            vv = T["v", g][:].rearrange("p a n -> p (a n)")
-            for lo, hi in [(0, D), (D, A * D)] if g == G - 1 else [(0, A * D)]:
-                nc.scalar.activation(out=u[:, lo:hi], in_=vv[:, lo:hi], func=ACT.Gelu)
-                nc.sync.dma_start(
-                    out=u_hbm[:, g * A * N_MLP + lo : g * A * N_MLP + hi],
-                    in_=u[:, lo:hi],
-                )
-
-        wpg = keep.tile([P, D, 4], BF16, name="wpg", align_bytes=64)
+        wg = keep.tile([P, D, 4], BF16, name="wg", tag="wg", align_bytes=64)
         wpc = keep.tile([P, D], U32, name="wpc", align_bytes=64)
         wpsc = keep.tile([P, D], U8, name="wpsc", align_bytes=64)
         gcols = keep.tile([P, 12], F32, name="gcols")
-        b1f = keep.tile([P, N_MLP], F32, name="b1f")
         w1p = keep.tile([P, 4, D], BF16, name="w1p")
-        w1g = keep.tile([P, N_MLP, 4], BF16, name="w1g", align_bytes=64)
         w1c = keep.tile([P, N_MLP], U32, name="w1c", align_bytes=64)
         w1sc = keep.tile([P, N_MLP], U8, name="w1sc", align_bytes=64)
+        sums = keep.tile([P, R], F32, name="sums")
+        ss = keep.tile([P, R], F32, name="ss")
+        std = keep.tile([P, R], F32, name="std")
+        nm = keep.tile([P, R], F32, name="nm")
+        rstd = keep.tile([P, R], F32, name="rstd")
+        nmr = keep.tile([P, R], F32, name="nmr")
+        T = {}
 
-        def st_WPT(h):
-            wpp = psum.tile([P, 2, 2, P], F32, name="wpp", tag="za" if h == 0 else "zb", bufs=1)
-            T["wpp", h] = wpp
+        def bank(tag, shape, dtype=F32):
+            b = psum.tile(shape, dtype, name=tag)
+            return b
+
+        def st_WPT(h, o):
+            T["wpp", h] = bank("q%d" % h, [P, 2, 2, P])
             for c in range(2):
                 words = wp[:, 2 * h + c, :].bitcast(F32)
                 for e in range(2):
-                    nc.tensor.transpose(wpp[:, c, e, :], words[:, e::2], ident[:])
+                    nc.tensor.transpose(T["wpp", h][:, c, e, :], words[:, e::2], ident[:])
 
-        def st_WPC(h):
+        def st_WPC(h, o):
             dst = (
-                wpg[:, h * 2 * P : (h + 1) * 2 * P, :]
+                wg[:, h * 2 * P : (h + 1) * 2 * P, :]
                 .rearrange("p n t -> p (n t)")
                 .bitcast(F32)
                 .rearrange("p (c n e) -> p c n e", c=2, e=2)
             )
             src = T["wpp", h][:].rearrange("p c e n -> p c n e")
-            if h == 0:
+            if o == 0:
                 nc.vector.tensor_copy(out=dst, in_=src)
             else:
                 nc.scalar.copy(out=dst, in_=src)
 
-        def st_WPQ(h):
-            nc.vector.quantize_mx(out=wpc[:].bitcast(FP8X4), scales=wpsc[:], in_=wpg[:].rearrange("p n t -> p (n t)"))
+        def st_WPQ(h, o):
+            nc.vector.quantize_mx(out=wpc[:].bitcast(FP8X4), scales=wpsc[:], in_=wg[:].rearrange("p n t -> p (n t)"))
 
-        def st_SC(h):
+        def st_SC(h, o):
             nc.vector.tensor_copy(out=scale[:, D : 2 * D], in_=scale[:, 0:D])
 
-        def st_GC(h):
-            gp = psum.tile([P, P], BF16, name="gp", tag="t0", bufs=1)
+        def st_GC(h, o):
+            gp = bank("r0", [P, P], BF16)
             nc.tensor.transpose(gp[:], grows[:], identb[:])
             nc.scalar.copy(out=gcols[:], in_=gp[:, 0:12])
 
-        def st_BB(h):
-            bb = psum.tile([P, N_MLP], F32, name="bb", tag="t1", bufs=1)
-            nc.tensor.matmul(out=bb[:], lhsT=identb[:, 0:1].to_broadcast([P, P]), rhs=vrows[:], start=True, stop=True)
-            nc.scalar.copy(out=b1f[:], in_=bb[:])
+        def st_DM(g, t):
+            mx(bank(t, [P, N_MLP])[:], (wpc, wpsc), slice(0, P), (wpc, wpsc), slice(0, D))
 
-        def st_W1P(c):
+        def st_W1P(c, o):
             nc.vector.tensor_copy(
                 out=w1p[:, c, :].rearrange("p (t b q) -> p t b q", t=4, q=8),
                 in_=w1[:, c, :].rearrange("p (b t q) -> p t b q", t=4, q=8),
             )
 
-        def st_W1T(h):
-            w1t = psum.tile([P, 2, 4, P], BF16, name="w1t", tag="za" if h == 0 else "zb", bufs=1)
+        def st_W1T(h, o):
+            w1t = bank("s%d" % h, [P, 2, 4, P], BF16)
             T["w1t", h] = w1t
             for c in range(2):
                 for t in range(4):
                     nc.tensor.transpose(w1t[:, c, t, :], w1p[:, 2 * h + c, t * P : (t + 1) * P], identb[:])
 
-        def st_W1C(h):
+        def st_W1C(h, o):
+            if "w1g" not in T:
+                w1g = keep.tile([P, N_MLP, 4], BF16, name="w1g", tag="wg", align_bytes=64)
+                T["w1g"] = w1g
+            w1g = T["w1g"]
             dst = w1g[:, h * 2 * P : (h + 1) * 2 * P, :].rearrange("p (c n) t -> p c n t", c=2)
-            nc.vector.tensor_copy(out=dst, in_=T["w1t", h][:].rearrange("p c t n -> p c n t"))
+            src = T["w1t", h][:].rearrange("p c t n -> p c n t")
+            if o == 0:
+                nc.vector.tensor_copy(out=dst, in_=src)
+            else:
+                nc.scalar.copy(out=dst, in_=src)
 
-        def st_W1Q(h):
-            nc.vector.quantize_mx(out=w1c[:].bitcast(FP8X4), scales=w1sc[:], in_=w1g[:].rearrange("p n t -> p (n t)"))
+        def st_W1Q(h, o):
+            nc.vector.quantize_mx(out=w1c[:].bitcast(FP8X4), scales=w1sc[:], in_=T["w1g"][:].rearrange("p n t -> p (n t)"))
+
+        def st_P(g, h):
+            if ("ab", g) not in T:
+                ab = work.tile([P, A * D], BF16, name="ab", tag="t4", align_bytes=64, bufs=3)
+                T["ab", g] = ab
+            r = g * A + 2 * h
+            i, c0 = where(r)
+            for lo, hi in [(0, D), (D, 2 * D)] if r == 0 else [(0, 2 * D)]:
+                nc.vector.tensor_tensor(
+                    out=T["ab", g][:, 2 * h * D + lo : 2 * h * D + hi],
+                    in0=byte_tiles[i][:, c0 + lo : c0 + hi].bitcast(FP8),
+                    in1=scale[:, 0 : hi - lo],
+                    op=ALU.mult,
+                )
+
+        def st_TA(g, h):
+            ta = bank("s%d" % h, [P, 2, 2, P])
+            T["ta", g, h] = ta
+            for a in range(2):
+                words = T["ab", g][:, (2 * h + a) * D : (2 * h + a + 1) * D].bitcast(F32)
+                for u in range(2):
+                    nc.tensor.transpose(ta[:, a, u, :], words[:, u::2], ident[:])
+
+        def st_CA(g, h):
+            if ("ag", g) not in T:
+                ag = work.tile([P, A, P, 4], BF16, name="ag", tag="t5", align_bytes=64)
+                T["ag", g] = ag
+            dst = (
+                T["ag", g][:, 2 * h : 2 * h + 2]
+                .rearrange("p a r f -> p a (r f)")
+                .bitcast(F32)
+                .rearrange("p a (r u) -> p a r u", u=2)
+            )
+            src = T["ta", g, h][:].rearrange("p a u r -> p a r u")
+            if 2 * g + h in CA_V:
+                nc.vector.tensor_copy(out=dst, in_=src)
+            else:
+                nc.scalar.copy(out=dst, in_=src)
+
+        def st_QA(g, h):
+            if ("ac", g) not in T:
+                ac = work.tile([P, A * P], U32, name="ac", tag="codes", align_bytes=64)
+                asc = work.tile([P, A * P], U8, name="asc", tag="planes", align_bytes=64)
+                T["ac", g] = (ac, asc)
+            lo, hi = (0, A) if h == 2 else (2 * h, 2 * h + 2)
+            nc.vector.quantize_mx(
+                out=T["ac", g][0][:, lo * P : hi * P].bitcast(FP8X4),
+                scales=T["ac", g][1][:, lo * P : hi * P],
+                in_=T["ag", g][:, lo:hi].rearrange("p a r f -> p (a r f)"),
+            )
+
+        def mx(out, lt, lc, rt, rc):
+            nc.tensor.matmul_mx(
+                out=out,
+                lhsT=lt[0][:, lc].bitcast(FP8X4),
+                lhsT_scale=lt[1][:, lc],
+                rhs=rt[0][:, rc].bitcast(FP8X4),
+                rhs_scale=rt[1][:, rc],
+                start=True,
+                stop=True,
+            )
+
+        def st_M1(g, f):
+            if ("m1", g, f // 2) not in T:
+                T["m1", g, f // 2] = bank("q%d" % (f // 2), [P, 2, 2 * P])
+            mx(
+                T["m1", g, f // 2][:, f % 2, :],
+                (wpc, wpsc), slice(f * P, (f + 1) * P), T["ac", g], slice(0, 2 * P),
+            )
+
+        def st_OT(g, f):
+            if ("ot", g) not in T:
+                ot = work.tile([P, 4, 2 * P], F32, name="ot")
+                T["ot", g] = ot
+            src = T["m1", g, f // 2][:, f % 2, :]
+            if 4 * g + f in OT_V:
+                nc.vector.tensor_scalar(
+                    out=T["ot", g][:, f, :], in0=src, scalar1=gcols[:, 8 + f : 9 + f], scalar2=None, op0=ALU.add
+                )
+            else:
+                nc.scalar.activation(
+                    out=T["ot", g][:, f, :], in_=src, func=ACT.Identity, bias=gcols[:, 8 + f : 9 + f]
+                )
+
+        def st_TO(g, a):
+            t = bank("r%d" % (a % 2), [P, D])
+            T["to", g, a] = t
+            if a >= 2:
+                mx(t[:], T["ac", g], slice(a * P, (a + 1) * P), (wpc, wpsc), slice(0, D))
+                return
+            for f in range(4):
+                nc.tensor.transpose(t[:, f * P : (f + 1) * P], T["ot", g][:, f, a * P : (a + 1) * P], ident[:])
+
+        def st_XP(g, a):
+            if g * A + a in XB_V:
+                return
+            i, c0 = where(g * A + a)
+            q = bank("q%d" % a, [P, D])
+            T["xp", g, a] = q
+            nc.tensor.matmul(out=q[:], lhsT=identb[:], rhs=x_tiles[i][:, c0 : c0 + D], start=True, stop=False)
+            nc.tensor.matmul(
+                out=q[:], lhsT=identb[:, 0:1].to_broadcast([P, P]), rhs=vrows[:], start=False, stop=True
+            )
+
+        def st_XE(g, a):
+            xb = work.tile([P, D], F32, name="xb", bufs=4)
+            T["xb", g, a] = xb
+            if g * A + a in XB_V:
+                i, c0 = where(g * A + a)
+                nc.vector.tensor_tensor(out=xb[:], in0=x_tiles[i][:, c0 : c0 + D], in1=bp[:], op=ALU.add)
+            else:
+                nc.scalar.copy(out=xb[:], in_=T["xp", g, a][:])
+
+        def st_XA(g, a):
+            if ("xm", g) not in T:
+                xm = keep.tile([P, A, D], F32, name="xm%d" % g)
+                T["xm", g] = xm
+            r = g * A + a
+            i, c0 = where(r)
+            nc.vector.scalar_tensor_tensor(
+                out=T["xm", g][:, a, :],
+                in0=T["to", g, a][:],
+                scalar=1.0,
+                in1=x_tiles[i][:, c0 : c0 + D] if a < 2 else T["xb", g, a][:],
+                op0=ALU.mult,
+                op1=ALU.add,
+                accum_out=sums[:, r : r + 1],
+            )
+            if a % 2 == 1:
+                nc.sync.dma_start(
+                    out=xm_hbm[:, (r - 1) * D : (r + 1) * D],
+                    in_=T["xm", g][:, a - 1 : a + 1, :].rearrange("p a d -> p (a d)"),
+                )
+
+        def st_SQ(g, a):
+            r = g * A + a
+            junk = work.tile([P, D], BF16, name="junk")
+            nc.scalar.activation(
+                out=junk[:],
+                in_=T["xm", g][:, a, :],
+                func=ACT.Square,
+                scale=-float(D),
+                bias=sums[:, r : r + 1],
+                accum_out=ss[:, r : r + 1],
+            )
+
+        def st_RS(g0, g1):
+            c = slice(g0 * A, g1 * A)
+            nc.scalar.activation(out=std[:, c], in_=ss[:, c], func=ACT.Sqrt, scale=1.0 / D**3, bias=epsc[:, 0:1])
+
+        def st_RV(g0, g1):
+            c = slice(g0 * A, g1 * A)
+            nc.vector.reciprocal(out=rstd[:, c], in_=std[:, c])
+            nc.vector.tensor_scalar(out=nm[:, c], in0=sums[:, c], scalar1=-1.0 / D, scalar2=None, op0=ALU.mult)
+            nc.vector.tensor_tensor(out=nmr[:, c], in0=nm[:, c], in1=rstd[:, c], op=ALU.mult)
+
+        def st_Z(g, a):
+            if ("z", g) not in T:
+                z = work.tile([P, A, D], F32, name="z", tag="big")
+                T["z", g] = z
+            r = g * A + a
+            src = T["xm", g][:, a, :].rearrange("p (b t q) -> p t b q", t=4, q=8)
+            dst = T["z", g][:, a, :].rearrange("p (t b q) -> p t b q", t=4, q=8)
+            if r in Z_S:
+                nc.scalar.activation(
+                    out=dst, in_=src, func=ACT.Identity, scale=rstd[:, r : r + 1], bias=nmr[:, r : r + 1]
+                )
+            else:
+                nc.vector.tensor_scalar(
+                    out=dst, in0=src, scalar1=nm[:, r : r + 1], scalar2=rstd[:, r : r + 1], op0=ALU.add, op1=ALU.mult
+                )
+
+        def st_TZ(g, a):
+            if ("zp", g) not in T:
+                T["zp", g] = [bank("q%d" % t, [P, A, P]) for t in range(4)]
+            for t in range(4):
+                nc.tensor.transpose(T["zp", g][t][:, a, :], T["z", g][:, a, t * P : (t + 1) * P], ident[:])
+
+        def st_PL(g, t):
+            if ("hp", g) not in T:
+                hp = work.tile([P, 4, A * P], BF16, name="hp", tag="t4", align_bytes=64, bufs=3)
+                T["hp", g] = hp
+            src = T["zp", g][t][:].rearrange("p a r -> p (a r)")
+            if 4 * g + t in PL_V:
+                nc.vector.tensor_scalar(
+                    out=T["hp", g][:, t, :],
+                    in0=src,
+                    scalar1=gcols[:, t : t + 1],
+                    scalar2=gcols[:, 4 + t : 5 + t],
+                    op0=ALU.mult,
+                    op1=ALU.add,
+                )
+            else:
+                nc.scalar.activation(
+                    out=T["hp", g][:, t, :],
+                    in_=src,
+                    func=ACT.Identity,
+                    scale=gcols[:, t : t + 1],
+                    bias=gcols[:, 4 + t : 5 + t],
+                )
+
+        def st_IL(g, h):
+            if ("hg", g) not in T:
+                hg = work.tile([P, A * P, 4], BF16, name="hg", tag="t5", align_bytes=64)
+                T["hg", g] = hg
+            lo, hi = (0, A * P) if h == 2 else (2 * h * P, 2 * (h + 1) * P)
+            nc.vector.tensor_copy(
+                out=T["hg", g][:, lo:hi, :].rearrange("p (c i) t -> p c t i", i=4),
+                in_=T["hp", g][:, :, lo:hi].rearrange("p t (c i) -> p c t i", i=4),
+            )
+
+        def st_QH(g, h):
+            if ("hc", g) not in T:
+                hc = work.tile([P, A * P], U32, name="hc", tag="codes", align_bytes=64)
+                hsc = work.tile([P, A * P], U8, name="hsc", tag="planes", align_bytes=64)
+                T["hc", g] = (hc, hsc)
+            lo, hi = (0, A * P) if h == 2 else (2 * h * P, 2 * (h + 1) * P)
+            nc.vector.quantize_mx(
+                out=T["hc", g][0][:, lo:hi].bitcast(FP8X4),
+                scales=T["hc", g][1][:, lo:hi],
+                in_=T["hg", g][:, lo:hi, :].rearrange("p r t -> p (r t)"),
+            )
+
+        def st_M2(g, a):
+            m = bank(("r0", "r1", "s0", "s1")[a], [P, N_MLP])
+            T["m2", g, a] = m
+            mx(m[:], T["hc", g], slice(a * P, (a + 1) * P), (w1c, w1sc), slice(0, N_MLP))
+
+        def st_B1(g, a):
+            if ("v", g) not in T:
+                v = work.tile([P, A, N_MLP], F32, name="v", bufs=3)
+                T["v", g] = v
+            nc.vector.tensor_tensor(out=T["v", g][:, a, :], in0=T["m2", g, a][:], in1=b1f[:], op=ALU.add)
+
+        def st_GE(g, h):
+            lo, hi = {0: (0, 2), 1: (2, 4), 2: (0, 4), 4: (0, 1), 5: (1, 2), 6: (2, 3), 7: (3, 4)}[h]
+            v = T["v", g][:, lo:hi, :].rearrange("p a n -> p (a n)")
+            nc.scalar.activation(out=v, in_=v, func=ACT.Gelu)
+            nc.sync.dma_start(out=u_hbm[:, (g * A + lo) * N_MLP : (g * A + hi) * N_MLP], in_=v)
 
         STAGES = {
+            "WPT": st_WPT, "WPC": st_WPC, "WPQ": st_WPQ, "SC": st_SC, "GC": st_GC, "DM": st_DM, "XP": st_XP, "XE": st_XE,
+            "W1P": st_W1P, "W1T": st_W1T, "W1C": st_W1C, "W1Q": st_W1Q,
             "P": st_P, "TA": st_TA, "CA": st_CA, "QA": st_QA, "M1": st_M1, "OT": st_OT, "TO": st_TO,
-            "NM": st_NM, "SQ": st_SQ, "RS": st_RS, "PL": st_PL, "IL": st_IL, "QH": st_QH, "GE": st_GE,
-            "DM": st_DM, "WPT": st_WPT, "WPC": st_WPC, "WPQ": st_WPQ, "SC": st_SC, "GC": st_GC, "BB": st_BB,
-            "W1P": st_W1P, "W1T": st_W1T, "W1C": st_W1C, "W1Q": st_W1Q, "DT": st_DT, "DZ": st_DZ, "DD": st_DD,
+            "XA": st_XA, "SQ": st_SQ, "RS": st_RS, "RV": st_RV,
+            "Z": st_Z, "TZ": st_TZ, "PL": st_PL, "IL": st_IL, "QH": st_QH, "M2": st_M2, "B1": st_B1, "GE": st_GE,
         }
-        PARTS = {"XA": st_XA, "Z": st_Z, "TZ": st_TZ, "M2": st_M2, "B1": st_B1}
-
-        def call(name, g):
-            if name[-1] in "01" and name[:-1] in PARTS:
-                PARTS[name[:-1]](g, int(name[-1]))
-            else:
-                STAGES[name](g)
-
-        for name, g in HEAD:
-            call(name, g)
-        for k in range(KFIRST, G + 4):
-            for name, off in TAIL.get(k, ORDER):
-                if 0 <= k + off < G:
-                    call(name, k + off)
+        for name, g, part in PROGRAM:
+            STAGES[name](g, part)

from contextlib import ExitStack

import concourse.mybir as mybir
from concourse.masks import make_identity

TOKENS, D, N_MLP = 4096, 512, 512
FLOPS = 2 * TOKENS * D * (D + N_MLP)
LN_EPS = 1e-6

F32 = mybir.dt.float32
BF16 = mybir.dt.bfloat16
U32 = mybir.dt.uint32
U8 = mybir.dt.uint8
FP8 = mybir.dt.float8_e4m3fn
FP8X4 = mybir.dt.float8_e4m3fn_x4
ACT = mybir.ActivationFunctionType
ALU = mybir.AluOpType

P = 128
R = TOKENS // P
A = 4
G = R // A
PROGRAM = [('WPT', 0, 0), ('WPT', 1, 0), ('SC', 0, 0), ('GC', 0, 0), ('WPC', 0, 0), ('P', 0, 0), ('WPC', 1, 1), ('P', 0, 1), ('TA', 0, 0), ('TA', 0, 1), ('P', 1, 0), ('CA', 0, 0), ('WPQ', 0, 0), ('CA', 0, 1), ('XP', 0, 2), ('P', 1, 1), ('TA', 1, 0), ('QA', 0, 2), ('TA', 1, 1), ('M1', 0, 3), ('M1', 0, 2), ('P', 2, 0), ('M1', 0, 0), ('M1', 0, 1), ('XE', 0, 2), ('CA', 1, 0), ('OT', 0, 3), ('CA', 1, 1), ('OT', 0, 0), ('XP', 0, 3), ('OT', 0, 1), ('P', 2, 1), ('TA', 2, 0), ('OT', 0, 2), ('XP', 1, 2), ('TO', 0, 0), ('TA', 2, 1), ('QA', 1, 2), ('XE', 0, 3), ('P', 3, 0), ('M1', 1, 3), ('M1', 1, 2), ('M1', 1, 0), ('TO', 0, 1), ('CA', 2, 0), ('XA', 0, 0), ('M1', 1, 1), ('XE', 1, 2), ('CA', 2, 1), ('XA', 0, 1), ('OT', 1, 3), ('TO', 0, 2), ('XA', 0, 2), ('P', 3, 1), ('OT', 1, 0), ('XP', 1, 3), ('TA', 3, 0), ('TO', 0, 3), ('OT', 1, 1), ('SQ', 0, 0), ('XP', 2, 2), ('XA', 0, 3), ('SQ', 0, 1), ('QA', 2, 2), ('OT', 1, 2), ('TA', 3, 1), ('TO', 1, 0), ('P', 4, 0), ('M1', 2, 3), ('M1', 2, 2), ('XE', 1, 3), ('M1', 2, 0), ('M1', 2, 1), ('CA', 3, 0), ('SQ', 0, 2), ('SQ', 0, 3), ('XE', 2, 2), ('CA', 3, 1), ('TO', 1, 1), ('OT', 2, 3), ('XA', 1, 0), ('XA', 1, 1), ('OT', 2, 0), ('XP', 2, 3), ('OT', 2, 1), ('P', 4, 1), ('TA', 4, 0), ('TO', 1, 2), ('XA', 1, 2), ('XP', 3, 2), ('OT', 2, 2), ('TO', 1, 3), ('QA', 3, 2), ('SQ', 1, 0), ('TA', 4, 1), ('TO', 2, 0), ('XA', 1, 3), ('SQ', 1, 1), ('P', 5, 0), ('XE', 2, 3), ('M1', 3, 3), ('M1', 3, 2), ('M1', 3, 0), ('M1', 3, 1), ('CA', 4, 0), ('XE', 3, 2), ('TO', 2, 1), ('XA', 2, 0), ('CA', 4, 1), ('SQ', 1, 2), ('OT', 3, 3), ('SQ', 1, 3), ('XA', 2, 1), ('OT', 3, 0), ('XP', 3, 3), ('P', 5, 1), ('TO', 2, 2), ('OT', 3, 1), ('TA', 5, 0), ('XA', 2, 2), ('XP', 4, 2), ('TO', 2, 3), ('SQ', 2, 0), ('OT', 3, 2), ('QA', 4, 2), ('TA', 5, 1), ('XA', 2, 3), ('SQ', 2, 1), ('TO', 3, 0), ('P', 6, 0), ('M1', 4, 3), ('XE', 3, 3), ('M1', 4, 2), ('M1', 4, 0), ('M1', 4, 1), ('CA', 5, 0), ('XE', 4, 2), ('TO', 3, 1), ('CA', 5, 1), ('SQ', 2, 2), ('XA', 3, 0), ('SQ', 2, 3), ('OT', 4, 3), ('XA', 3, 1), ('OT', 4, 0), ('XP', 4, 3), ('P', 6, 1), ('OT', 4, 1), ('TA', 6, 0), ('TO', 3, 2), ('XA', 3, 2), ('XP', 5, 2), ('TO', 3, 3), ('OT', 4, 2), ('SQ', 3, 0), ('QA', 5, 2), ('TA', 6, 1), ('XA', 3, 3), ('SQ', 3, 1), ('TO', 4, 0), ('P', 7, 0), ('M1', 5, 3), ('XE', 4, 3), ('M1', 5, 2), ('M1', 5, 0), ('M1', 5, 1), ('CA', 6, 0), ('XE', 5, 2), ('TO', 4, 1), ('CA', 6, 1), ('XA', 4, 0), ('SQ', 3, 2), ('OT', 5, 3), ('SQ', 3, 3), ('XA', 4, 1), ('OT', 5, 0), ('XP', 5, 3), ('P', 7, 1), ('OT', 5, 1), ('TA', 7, 0), ('TO', 4, 2), ('XA', 4, 2), ('W1P', 2, 0), ('XP', 6, 2), ('TO', 4, 3), ('OT', 5, 2), ('SQ', 4, 0), ('QA', 6, 2), ('TA', 7, 1), ('XA', 4, 3), ('SQ', 4, 1), ('W1P', 0, 0), ('TO', 5, 0), ('W1P', 1, 0), ('M1', 6, 3), ('XE', 5, 3), ('M1', 6, 2), ('M1', 6, 0), ('M1', 6, 1), ('CA', 7, 0), ('XE', 6, 2), ('TO', 5, 1), ('CA', 7, 1), ('XA', 5, 0), ('SQ', 4, 2), ('OT', 6, 3), ('SQ', 4, 3), ('XA', 5, 1), ('OT', 6, 0), ('XP', 6, 3), ('OT', 6, 1), ('TO', 5, 2), ('XA', 5, 2), ('XP', 7, 2), ('TO', 5, 3), ('OT', 6, 2), ('SQ', 5, 0), ('QA', 7, 2), ('XA', 5, 3), ('SQ', 5, 1), ('TO', 6, 0), ('M1', 7, 3), ('XE', 6, 3), ('M1', 7, 2), ('M1', 7, 0), ('M1', 7, 1), ('XE', 7, 2), ('TO', 6, 1), ('XA', 6, 0), ('SQ', 5, 2), ('OT', 7, 3), ('SQ', 5, 3), ('W1P', 3, 0), ('XA', 6, 1), ('OT', 7, 0), ('XP', 7, 3), ('OT', 7, 1), ('TO', 6, 2), ('XA', 6, 2), ('TO', 6, 3), ('OT', 7, 2), ('SQ', 6, 0), ('XA', 6, 3), ('SQ', 6, 1), ('TO', 7, 0), ('XE', 7, 3), ('RS', 0, 6), ('TO', 7, 1), ('XA', 7, 0), ('SQ', 6, 2), ('SQ', 6, 3), ('XA', 7, 1), ('TO', 7, 2), ('XA', 7, 2), ('TO', 7, 3), ('SQ', 7, 0), ('XA', 7, 3), ('SQ', 7, 1), ('RV', 0, 6), ('SQ', 7, 2), ('SQ', 7, 3), ('W1T', 1, 0), ('W1T', 0, 0), ('Z', 0, 1), ('Z', 0, 0), ('Z', 0, 2), ('RS', 6, 8), ('Z', 1, 1), ('Z', 1, 0), ('Z', 0, 3), ('TZ', 0, 1), ('TZ', 0, 0), ('W1C', 1, 0), ('W1C', 0, 0), ('Z', 1, 2), ('TZ', 0, 2), ('TZ', 0, 3), ('Z', 2, 1), ('Z', 2, 0), ('Z', 1, 3), ('PL', 0, 0), ('PL', 0, 2), ('PL', 0, 1), ('PL', 0, 3), ('TZ', 1, 1), ('TZ', 1, 0), ('W1Q', 0, 0), ('Z', 2, 2), ('TZ', 1, 2), ('IL', 0, 2), ('TZ', 1, 3), ('QH', 0, 2), ('Z', 3, 1), ('Z', 3, 0), ('Z', 2, 3), ('RV', 6, 8), ('PL', 1, 0), ('PL', 1, 2), ('M2', 0, 0), ('PL', 1, 1), ('PL', 1, 3), ('TZ', 2, 1), ('TZ', 2, 0), ('Z', 3, 2), ('TZ', 2, 2), ('IL', 1, 2), ('TZ', 2, 3), ('QH', 1, 2), ('M2', 0, 1), ('B1', 0, 0), ('Z', 4, 1), ('Z', 4, 0), ('Z', 3, 3), ('M2', 0, 2), ('B1', 0, 1), ('PL', 2, 0), ('B1', 0, 2), ('PL', 2, 2), ('M2', 0, 3), ('M2', 1, 0), ('PL', 2, 1), ('PL', 2, 3), ('TZ', 3, 1), ('TZ', 3, 0), ('Z', 4, 2), ('TZ', 3, 2), ('IL', 2, 2), ('B1', 0, 3), ('TZ', 3, 3), ('QH', 2, 2), ('M2', 1, 1), ('B1', 1, 0), ('Z', 5, 1), ('Z', 5, 0), ('Z', 4, 3), ('M2', 1, 2), ('B1', 1, 1), ('PL', 3, 0), ('B1', 1, 2), ('PL', 3, 2), ('M2', 1, 3), ('M2', 2, 0), ('PL', 3, 1), ('PL', 3, 3), ('TZ', 4, 1), ('TZ', 4, 0), ('Z', 5, 2), ('TZ', 4, 2), ('IL', 3, 2), ('B1', 1, 3), ('TZ', 4, 3), ('QH', 3, 2), ('M2', 2, 1), ('B1', 2, 0), ('Z', 6, 1), ('Z', 6, 0), ('GE', 0, 2), ('Z', 5, 3), ('M2', 2, 2), ('B1', 2, 1), ('PL', 4, 0), ('B1', 2, 2), ('PL', 4, 2), ('M2', 2, 3), ('M2', 3, 0), ('PL', 4, 1), ('PL', 4, 3), ('TZ', 5, 1), ('TZ', 5, 0), ('Z', 6, 2), ('TZ', 5, 2), ('IL', 4, 2), ('B1', 2, 3), ('TZ', 5, 3), ('QH', 4, 2), ('M2', 3, 1), ('B1', 3, 0), ('Z', 7, 1), ('Z', 7, 0), ('GE', 1, 2), ('Z', 6, 3), ('M2', 3, 2), ('B1', 3, 1), ('PL', 5, 0), ('B1', 3, 2), ('PL', 5, 2), ('M2', 3, 3), ('M2', 4, 0), ('PL', 5, 1), ('PL', 5, 3), ('TZ', 6, 1), ('TZ', 6, 0), ('Z', 7, 2), ('TZ', 6, 2), ('IL', 5, 2), ('B1', 3, 3), ('TZ', 6, 3), ('QH', 5, 2), ('M2', 4, 1), ('B1', 4, 0), ('GE', 2, 2), ('Z', 7, 3), ('M2', 4, 2), ('B1', 4, 1), ('PL', 6, 0), ('B1', 4, 2), ('PL', 6, 2), ('M2', 4, 3), ('M2', 5, 0), ('PL', 6, 1), ('PL', 6, 3), ('TZ', 7, 1), ('TZ', 7, 0), ('TZ', 7, 2), ('IL', 6, 2), ('B1', 4, 3), ('TZ', 7, 3), ('QH', 6, 2), ('M2', 5, 1), ('B1', 5, 0), ('GE', 3, 2), ('M2', 5, 2), ('B1', 5, 1), ('PL', 7, 0), ('B1', 5, 2), ('PL', 7, 2), ('M2', 5, 3), ('M2', 6, 0), ('PL', 7, 1), ('PL', 7, 3), ('IL', 7, 2), ('B1', 5, 3), ('QH', 7, 2), ('M2', 6, 1), ('B1', 6, 0), ('GE', 4, 2), ('M2', 6, 2), ('B1', 6, 1), ('B1', 6, 2), ('M2', 6, 3), ('M2', 7, 0), ('B1', 6, 3), ('M2', 7, 1), ('B1', 7, 0), ('GE', 5, 2), ('M2', 7, 2), ('B1', 7, 1), ('B1', 7, 2), ('M2', 7, 3), ('B1', 7, 3), ('GE', 6, 2), ('GE', 7, 0), ('GE', 7, 1)]
OT_V = set()
PL_V = set()
Z_S = {2, 3, 7, 10, 11, 15, 18, 19, 23, 26, 27, 31}
CA_V = set()
XB_V = {11, 19, 3, 27}
CHUNKS = [2, 2, 4, 8, 8, 8]


def tile_block_pb_t_kernel(
    tc, attn_out_bytes, attn_out_scale, x, W_proj, b_proj, g2, beta2, W1, b1, out_0, out_1
):
    nc = tc.nc
    bytes_hbm = attn_out_bytes.rearrange("b s d -> (b s) d").rearrange("(p r) d -> p (r d)", p=P)
    x_hbm = x.rearrange("b s d -> (b s) d").rearrange("(p r) d -> p (r d)", p=P)
    xm_hbm = out_0.rearrange("b s d -> (b s) d").rearrange("(p r) d -> p (r d)", p=P)
    u_hbm = out_1.rearrange("b s d -> (b s) d").rearrange("(p r) d -> p (r d)", p=P)

    with ExitStack() as ctx:
        keep = ctx.enter_context(tc.tile_pool(name="keep", bufs=1))
        work = ctx.enter_context(tc.tile_pool(name="work", bufs=2))
        psum = ctx.enter_context(tc.psum_pool(name="psum", bufs=1))
        ctx.enter_context(tc.manual_schedule())

        scale = keep.tile([P, 2 * D], F32, name="scale")
        nc.scalar.dma_start(out=scale[:, 0:D], in_=attn_out_scale.rearrange("a b k -> (a b k)").partition_broadcast(P))
        vrows = keep.tile([P, D], BF16, name="vrows")
        nc.vector.memset(vrows[:], 0.0)
        grows = keep.tile([P, P], BF16, name="grows")
        nc.vector.memset(grows[:], 0.0)
        dummy = keep.tile([P, 1], F32, name="dummy")
        nc.vector.memset(dummy[:], 1.0)
        epsc = keep.tile([P, 1], F32, name="epsc")
        nc.vector.tensor_scalar(out=epsc[:], in0=dummy[:], scalar1=LN_EPS, scalar2=None, op0=ALU.mult)
        ident = keep.tile([P, P], F32, name="ident")
        make_identity(nc, ident[:])
        identb = keep.tile([P, P], BF16, name="identb")
        nc.vector.tensor_copy(out=identb[:], in_=ident[:])
        nc.scalar.activation(out=dummy[:], in_=dummy[:], func=ACT.Sqrt)

        starts = [sum(CHUNKS[:i]) for i in range(len(CHUNKS))]
        byte_tiles = []
        x_tiles = []
        for i in range(len(CHUNKS)):
            bt = keep.tile([P, CHUNKS[i] * D], U8, name="bytes%d" % i, align_bytes=64)
            byte_tiles.append(bt)
            xt = keep.tile([P, CHUNKS[i] * D], BF16, name="xin%d" % i, align_bytes=64)
            x_tiles.append(xt)

        def load_bytes(i):
            nc.sync.dma_start(out=byte_tiles[i][:], in_=bytes_hbm[:, starts[i] * D : (starts[i] + CHUNKS[i]) * D])

        def load_x(i):
            nc.sync.dma_start(out=x_tiles[i][:], in_=x_hbm[:, starts[i] * D : (starts[i] + CHUNKS[i]) * D])

        def where(r):
            i = max(j for j in range(len(CHUNKS)) if starts[j] <= r)
            return i, (r - starts[i]) * D

        wp = keep.tile([P, 4, D], BF16, name="wp")
        w1 = keep.tile([P, 4, D], BF16, name="w1")
        wp_hbm = W_proj.rearrange("(c p) k -> p c k", p=P)
        load_bytes(0)
        nc.sync.dma_start(out=wp[:, 0:2, :], in_=wp_hbm[:, 0:2, :])
        nc.sync.dma_start(out=wp[:, 2:4, :], in_=wp_hbm[:, 2:4, :])
        nc.sync.dma_start(
            out=grows[0:4, :].rearrange("t (b q) -> t b q", q=8), in_=g2.rearrange("(b t q) -> t b q", t=4, q=8)
        )
        nc.sync.dma_start(
            out=grows[4:8, :].rearrange("t (b q) -> t b q", q=8), in_=beta2.rearrange("(b t q) -> t b q", t=4, q=8)
        )
        nc.sync.dma_start(out=grows[8:12, :], in_=b_proj.rearrange("(f p) -> f p", p=P))
        nc.sync.dma_start(out=vrows[0:1, :], in_=b_proj.rearrange("(o k) -> o k", o=1))
        load_bytes(1)
        load_x(0)
        bp = keep.tile([P, D], BF16, name="bp")
        nc.sync.dma_start(out=bp[:], in_=b_proj.partition_broadcast(P))
        load_bytes(2)
        load_x(1)
        load_bytes(3)
        load_x(2)
        load_x(3)
        nc.sync.dma_start(out=w1[:], in_=W1.rearrange("(c p) k -> p c k", p=P))
        b1f = keep.tile([P, N_MLP], BF16, name="b1f")
        nc.sync.dma_start(out=b1f[:], in_=b1.partition_broadcast(P))
        for i in range(4, len(CHUNKS)):
            load_bytes(i)
            load_x(i)

        wg = keep.tile([P, D, 4], BF16, name="wg", tag="wg", align_bytes=64)
        wpc = keep.tile([P, D], U32, name="wpc", align_bytes=64)
        wpsc = keep.tile([P, D], U8, name="wpsc", align_bytes=64)
        gcols = keep.tile([P, 12], F32, name="gcols")
        w1p = keep.tile([P, 4, D], BF16, name="w1p")
        w1c = keep.tile([P, N_MLP], U32, name="w1c", align_bytes=64)
        w1sc = keep.tile([P, N_MLP], U8, name="w1sc", align_bytes=64)
        sums = keep.tile([P, R], F32, name="sums")
        ss = keep.tile([P, R], F32, name="ss")
        std = keep.tile([P, R], F32, name="std")
        nm = keep.tile([P, R], F32, name="nm")
        rstd = keep.tile([P, R], F32, name="rstd")
        nmr = keep.tile([P, R], F32, name="nmr")
        T = {}

        def bank(tag, shape, dtype=F32):
            b = psum.tile(shape, dtype, name=tag)
            return b

        def st_WPT(h, o):
            T["wpp", h] = bank("q%d" % h, [P, 2, 2, P])
            for c in range(2):
                words = wp[:, 2 * h + c, :].bitcast(F32)
                for e in range(2):
                    nc.tensor.transpose(T["wpp", h][:, c, e, :], words[:, e::2], ident[:])

        def st_WPC(h, o):
            dst = (
                wg[:, h * 2 * P : (h + 1) * 2 * P, :]
                .rearrange("p n t -> p (n t)")
                .bitcast(F32)
                .rearrange("p (c n e) -> p c n e", c=2, e=2)
            )
            src = T["wpp", h][:].rearrange("p c e n -> p c n e")
            if o == 0:
                nc.vector.tensor_copy(out=dst, in_=src)
            else:
                nc.scalar.copy(out=dst, in_=src)

        def st_WPQ(h, o):
            nc.vector.quantize_mx(out=wpc[:].bitcast(FP8X4), scales=wpsc[:], in_=wg[:].rearrange("p n t -> p (n t)"))

        def st_SC(h, o):
            nc.vector.tensor_copy(out=scale[:, D : 2 * D], in_=scale[:, 0:D])

        def st_GC(h, o):
            gp = bank("r0", [P, P], BF16)
            nc.tensor.transpose(gp[:], grows[:], identb[:])
            nc.scalar.copy(out=gcols[:], in_=gp[:, 0:12])

        def st_DM(g, t):
            mx(bank(t, [P, N_MLP])[:], (wpc, wpsc), slice(0, P), (wpc, wpsc), slice(0, D))

        def st_W1P(c, o):
            nc.vector.tensor_copy(
                out=w1p[:, c, :].rearrange("p (t b q) -> p t b q", t=4, q=8),
                in_=w1[:, c, :].rearrange("p (b t q) -> p t b q", t=4, q=8),
            )

        def st_W1T(h, o):
            w1t = bank("s%d" % h, [P, 2, 4, P], BF16)
            T["w1t", h] = w1t
            for c in range(2):
                for t in range(4):
                    nc.tensor.transpose(w1t[:, c, t, :], w1p[:, 2 * h + c, t * P : (t + 1) * P], identb[:])

        def st_W1C(h, o):
            if "w1g" not in T:
                w1g = keep.tile([P, N_MLP, 4], BF16, name="w1g", tag="wg", align_bytes=64)
                T["w1g"] = w1g
            w1g = T["w1g"]
            dst = w1g[:, h * 2 * P : (h + 1) * 2 * P, :].rearrange("p (c n) t -> p c n t", c=2)
            src = T["w1t", h][:].rearrange("p c t n -> p c n t")
            if o == 0:
                nc.vector.tensor_copy(out=dst, in_=src)
            else:
                nc.scalar.copy(out=dst, in_=src)

        def st_W1Q(h, o):
            nc.vector.quantize_mx(out=w1c[:].bitcast(FP8X4), scales=w1sc[:], in_=T["w1g"][:].rearrange("p n t -> p (n t)"))

        def st_P(g, h):
            if ("ab", g) not in T:
                ab = work.tile([P, A * D], BF16, name="ab", tag="t4", align_bytes=64, bufs=3)
                T["ab", g] = ab
            r = g * A + 2 * h
            i, c0 = where(r)
            for lo, hi in [(0, D), (D, 2 * D)] if r == 0 else [(0, 2 * D)]:
                nc.vector.tensor_tensor(
                    out=T["ab", g][:, 2 * h * D + lo : 2 * h * D + hi],
                    in0=byte_tiles[i][:, c0 + lo : c0 + hi].bitcast(FP8),
                    in1=scale[:, 0 : hi - lo],
                    op=ALU.mult,
                )

        def st_TA(g, h):
            ta = bank("s%d" % h, [P, 2, 2, P])
            T["ta", g, h] = ta
            for a in range(2):
                words = T["ab", g][:, (2 * h + a) * D : (2 * h + a + 1) * D].bitcast(F32)
                for u in range(2):
                    nc.tensor.transpose(ta[:, a, u, :], words[:, u::2], ident[:])

        def st_CA(g, h):
            if ("ag", g) not in T:
                ag = work.tile([P, A, P, 4], BF16, name="ag", tag="t5", align_bytes=64)
                T["ag", g] = ag
            dst = (
                T["ag", g][:, 2 * h : 2 * h + 2]
                .rearrange("p a r f -> p a (r f)")
                .bitcast(F32)
                .rearrange("p a (r u) -> p a r u", u=2)
            )
            src = T["ta", g, h][:].rearrange("p a u r -> p a r u")
            if 2 * g + h in CA_V:
                nc.vector.tensor_copy(out=dst, in_=src)
            else:
                nc.scalar.copy(out=dst, in_=src)

        def st_QA(g, h):
            if ("ac", g) not in T:
                ac = work.tile([P, A * P], U32, name="ac", tag="codes", align_bytes=64)
                asc = work.tile([P, A * P], U8, name="asc", tag="planes", align_bytes=64)
                T["ac", g] = (ac, asc)
            lo, hi = (0, A) if h == 2 else (2 * h, 2 * h + 2)
            nc.vector.quantize_mx(
                out=T["ac", g][0][:, lo * P : hi * P].bitcast(FP8X4),
                scales=T["ac", g][1][:, lo * P : hi * P],
                in_=T["ag", g][:, lo:hi].rearrange("p a r f -> p (a r f)"),
            )

        def mx(out, lt, lc, rt, rc):
            nc.tensor.matmul_mx(
                out=out,
                lhsT=lt[0][:, lc].bitcast(FP8X4),
                lhsT_scale=lt[1][:, lc],
                rhs=rt[0][:, rc].bitcast(FP8X4),
                rhs_scale=rt[1][:, rc],
                start=True,
                stop=True,
            )

        def st_M1(g, f):
            if ("m1", g, f // 2) not in T:
                T["m1", g, f // 2] = bank("q%d" % (f // 2), [P, 2, 2 * P])
            mx(
                T["m1", g, f // 2][:, f % 2, :],
                (wpc, wpsc), slice(f * P, (f + 1) * P), T["ac", g], slice(0, 2 * P),
            )

        def st_OT(g, f):
            if ("ot", g) not in T:
                ot = work.tile([P, 4, 2 * P], F32, name="ot")
                T["ot", g] = ot
            src = T["m1", g, f // 2][:, f % 2, :]
            if 4 * g + f in OT_V:
                nc.vector.tensor_scalar(
                    out=T["ot", g][:, f, :], in0=src, scalar1=gcols[:, 8 + f : 9 + f], scalar2=None, op0=ALU.add
                )
            else:
                nc.scalar.activation(
                    out=T["ot", g][:, f, :], in_=src, func=ACT.Identity, bias=gcols[:, 8 + f : 9 + f]
                )

        def st_TO(g, a):
            t = bank("r%d" % (a % 2), [P, D])
            T["to", g, a] = t
            if a >= 2:
                mx(t[:], T["ac", g], slice(a * P, (a + 1) * P), (wpc, wpsc), slice(0, D))
                return
            for f in range(4):
                nc.tensor.transpose(t[:, f * P : (f + 1) * P], T["ot", g][:, f, a * P : (a + 1) * P], ident[:])

        def st_XP(g, a):
            if g * A + a in XB_V:
                return
            i, c0 = where(g * A + a)
            q = bank("q%d" % a, [P, D])
            T["xp", g, a] = q
            nc.tensor.matmul(out=q[:], lhsT=identb[:], rhs=x_tiles[i][:, c0 : c0 + D], start=True, stop=False)
            nc.tensor.matmul(
                out=q[:], lhsT=identb[:, 0:1].to_broadcast([P, P]), rhs=vrows[:], start=False, stop=True
            )

        def st_XE(g, a):
            xb = work.tile([P, D], F32, name="xb", bufs=4)
            T["xb", g, a] = xb
            if g * A + a in XB_V:
                i, c0 = where(g * A + a)
                nc.vector.tensor_tensor(out=xb[:], in0=x_tiles[i][:, c0 : c0 + D], in1=bp[:], op=ALU.add)
            else:
                nc.scalar.copy(out=xb[:], in_=T["xp", g, a][:])

        def st_XA(g, a):
            if ("xm", g) not in T:
                xm = keep.tile([P, A, D], F32, name="xm%d" % g)
                T["xm", g] = xm
            r = g * A + a
            i, c0 = where(r)
            nc.vector.scalar_tensor_tensor(
                out=T["xm", g][:, a, :],
                in0=T["to", g, a][:],
                scalar=1.0,
                in1=x_tiles[i][:, c0 : c0 + D] if a < 2 else T["xb", g, a][:],
                op0=ALU.mult,
                op1=ALU.add,
                accum_out=sums[:, r : r + 1],
            )
            if a % 2 == 1:
                nc.sync.dma_start(
                    out=xm_hbm[:, (r - 1) * D : (r + 1) * D],
                    in_=T["xm", g][:, a - 1 : a + 1, :].rearrange("p a d -> p (a d)"),
                )

        def st_SQ(g, a):
            r = g * A + a
            junk = work.tile([P, D], BF16, name="junk")
            nc.scalar.activation(
                out=junk[:],
                in_=T["xm", g][:, a, :],
                func=ACT.Square,
                scale=-float(D),
                bias=sums[:, r : r + 1],
                accum_out=ss[:, r : r + 1],
            )

        def st_RS(g0, g1):
            c = slice(g0 * A, g1 * A)
            nc.scalar.activation(out=std[:, c], in_=ss[:, c], func=ACT.Sqrt, scale=1.0 / D**3, bias=epsc[:, 0:1])

        def st_RV(g0, g1):
            c = slice(g0 * A, g1 * A)
            nc.vector.reciprocal(out=rstd[:, c], in_=std[:, c])
            nc.vector.tensor_scalar(out=nm[:, c], in0=sums[:, c], scalar1=-1.0 / D, scalar2=None, op0=ALU.mult)
            nc.vector.tensor_tensor(out=nmr[:, c], in0=nm[:, c], in1=rstd[:, c], op=ALU.mult)

        def st_Z(g, a):
            if ("z", g) not in T:
                z = work.tile([P, A, D], F32, name="z", tag="big")
                T["z", g] = z
            r = g * A + a
            src = T["xm", g][:, a, :].rearrange("p (b t q) -> p t b q", t=4, q=8)
            dst = T["z", g][:, a, :].rearrange("p (t b q) -> p t b q", t=4, q=8)
            if r in Z_S:
                nc.scalar.activation(
                    out=dst, in_=src, func=ACT.Identity, scale=rstd[:, r : r + 1], bias=nmr[:, r : r + 1]
                )
            else:
                nc.vector.tensor_scalar(
                    out=dst, in0=src, scalar1=nm[:, r : r + 1], scalar2=rstd[:, r : r + 1], op0=ALU.add, op1=ALU.mult
                )

        def st_TZ(g, a):
            if ("zp", g) not in T:
                T["zp", g] = [bank("q%d" % t, [P, A, P]) for t in range(4)]
            for t in range(4):
                nc.tensor.transpose(T["zp", g][t][:, a, :], T["z", g][:, a, t * P : (t + 1) * P], ident[:])

        def st_PL(g, t):
            if ("hp", g) not in T:
                hp = work.tile([P, 4, A * P], BF16, name="hp", tag="t4", align_bytes=64, bufs=3)
                T["hp", g] = hp
            src = T["zp", g][t][:].rearrange("p a r -> p (a r)")
            if 4 * g + t in PL_V:
                nc.vector.tensor_scalar(
                    out=T["hp", g][:, t, :],
                    in0=src,
                    scalar1=gcols[:, t : t + 1],
                    scalar2=gcols[:, 4 + t : 5 + t],
                    op0=ALU.mult,
                    op1=ALU.add,
                )
            else:
                nc.scalar.activation(
                    out=T["hp", g][:, t, :],
                    in_=src,
                    func=ACT.Identity,
                    scale=gcols[:, t : t + 1],
                    bias=gcols[:, 4 + t : 5 + t],
                )

        def st_IL(g, h):
            if ("hg", g) not in T:
                hg = work.tile([P, A * P, 4], BF16, name="hg", tag="t5", align_bytes=64)
                T["hg", g] = hg
            lo, hi = (0, A * P) if h == 2 else (2 * h * P, 2 * (h + 1) * P)
            nc.vector.tensor_copy(
                out=T["hg", g][:, lo:hi, :].rearrange("p (c i) t -> p c t i", i=4),
                in_=T["hp", g][:, :, lo:hi].rearrange("p t (c i) -> p c t i", i=4),
            )

        def st_QH(g, h):
            if ("hc", g) not in T:
                hc = work.tile([P, A * P], U32, name="hc", tag="codes", align_bytes=64)
                hsc = work.tile([P, A * P], U8, name="hsc", tag="planes", align_bytes=64)
                T["hc", g] = (hc, hsc)
            lo, hi = (0, A * P) if h == 2 else (2 * h * P, 2 * (h + 1) * P)
            nc.vector.quantize_mx(
                out=T["hc", g][0][:, lo:hi].bitcast(FP8X4),
                scales=T["hc", g][1][:, lo:hi],
                in_=T["hg", g][:, lo:hi, :].rearrange("p r t -> p (r t)"),
            )

        def st_M2(g, a):
            m = bank(("r0", "r1", "s0", "s1")[a], [P, N_MLP])
            T["m2", g, a] = m
            mx(m[:], T["hc", g], slice(a * P, (a + 1) * P), (w1c, w1sc), slice(0, N_MLP))

        def st_B1(g, a):
            if ("v", g) not in T:
                v = work.tile([P, A, N_MLP], F32, name="v", bufs=3)
                T["v", g] = v
            nc.vector.tensor_tensor(out=T["v", g][:, a, :], in0=T["m2", g, a][:], in1=b1f[:], op=ALU.add)

        def st_GE(g, h):
            lo, hi = {0: (0, 2), 1: (2, 4), 2: (0, 4), 4: (0, 1), 5: (1, 2), 6: (2, 3), 7: (3, 4)}[h]
            v = T["v", g][:, lo:hi, :].rearrange("p a n -> p (a n)")
            nc.scalar.activation(out=v, in_=v, func=ACT.Gelu)
            nc.sync.dma_start(out=u_hbm[:, (g * A + lo) * N_MLP : (g * A + hi) * N_MLP], in_=v)

        STAGES = {
            "WPT": st_WPT, "WPC": st_WPC, "WPQ": st_WPQ, "SC": st_SC, "GC": st_GC, "DM": st_DM, "XP": st_XP, "XE": st_XE,
            "W1P": st_W1P, "W1T": st_W1T, "W1C": st_W1C, "W1Q": st_W1Q,
            "P": st_P, "TA": st_TA, "CA": st_CA, "QA": st_QA, "M1": st_M1, "OT": st_OT, "TO": st_TO,
            "XA": st_XA, "SQ": st_SQ, "RS": st_RS, "RV": st_RV,
            "Z": st_Z, "TZ": st_TZ, "PL": st_PL, "IL": st_IL, "QH": st_QH, "M2": st_M2, "B1": st_B1, "GE": st_GE,
        }
        for name, g, part in PROGRAM:
            STAGES[name](g, part)
